import numpy as np
import ml_dtypes


def mxq(x, axis, fmt="e4m3"):
    dtype, down = {"e4m3": (ml_dtypes.float8_e4m3fn, 7), "e5m2": (ml_dtypes.float8_e5m2, 14)}[fmt]
    v = np.moveaxis(np.asarray(x, np.float32).astype(ml_dtypes.bfloat16).astype(np.float64), axis, -1)
    blocks = v.reshape(v.shape[:-1] + (-1, 32))
    amax = np.abs(blocks).max(-1, keepdims=True)
    byte = np.maximum(np.where(amax > 0, np.frexp(amax)[1] - 1 + 127, 0) - down, 1)
    scale = np.exp2(byte - 127.0)
    codes = (blocks / scale).astype(np.float32).astype(dtype).astype(np.float64)
    return np.moveaxis((codes * scale).reshape(v.shape), -1, axis)


WIDE = False


def mx_kscale(k):
    if not WIDE:
        return np.ones(k)
    levels = np.array([10, -10, 5, -5, 0])
    a = np.random.permutation(np.resize(levels, k // 512 * 4)).reshape(k // 512, 4)
    idx = np.arange(k)
    return np.exp2(a[idx // 512, idx % 128 // 32])


BF16 = ml_dtypes.bfloat16


def bf(x):
    return np.asarray(x, np.float32).astype(BF16)


def f64(x):
    return np.asarray(x).astype(np.float64)


B, K, N = 16384, 512, 256


def setup_inputs():
    s = mx_kscale(K)
    return {"x": bf(np.random.standard_normal((B, K)) * s),
            "dft_real": bf(np.random.standard_normal((N, K)) / np.sqrt(K) / s[None, :]),
            "dft_imag": bf(np.random.standard_normal((N, K)) / np.sqrt(K) / s[None, :])}


def reference(x, dft_real, dft_imag):
    xq = mxq(f64(x), 1, "e4m3")
    rxs = xq @ mxq(f64(dft_real), 1, "e4m3").T
    ixs = xq @ mxq(f64(dft_imag), 1, "e4m3").T
    mag = np.log(rxs * rxs + ixs * ixs)
    return mag

@@ -1,0 +1,164 @@
+from contextlib import ExitStack
+
+import concourse.mybir as mybir
+from concourse.masks import make_identity
+
+F32 = mybir.dt.float32
+BF16 = mybir.dt.bfloat16
+U32 = mybir.dt.uint32
+U8 = mybir.dt.uint8
+FP8X4 = mybir.dt.float8_e4m3fn_x4
+ACT = mybir.ActivationFunctionType
+ALU = mybir.AluOpType
+
+P = 128
+B, K, N = 16384, 512, 256
+FLOPS = 2 * B * K * 2 * N
+
+CHUNK_BLOCKS = 8
+GROUP_BLOCKS = 4
+CHUNKS = B // (P * CHUNK_BLOCKS)
+GROUPS = B // (P * GROUP_BLOCKS)
+GROUPS_PER_CHUNK = CHUNK_BLOCKS // GROUP_BLOCKS
+WORDS = K // 2
+
+MANUAL = True
+
+
+def tile_dft_kernel(tc, x, dft_real, dft_imag, out):
+    nc = tc.nc
+    with ExitStack() as ctx:
+        const = ctx.enter_context(tc.tile_pool(name="const", bufs=1))
+        xpool = ctx.enter_context(tc.tile_pool(name="xpool", bufs=CHUNKS))
+        gpool = ctx.enter_context(tc.tile_pool(name="gpool", bufs=3))
+        qpool = ctx.enter_context(tc.tile_pool(name="qpool", bufs=3))
+        spool = ctx.enter_context(tc.tile_pool(name="spool", bufs=3))
+        opool = ctx.enter_context(tc.tile_pool(name="opool", bufs=3))
+        tpsum = ctx.enter_context(tc.psum_pool(name="tpsum", bufs=4))
+        zpsum = ctx.enter_context(tc.psum_pool(name="zpsum", bufs=4))
+        if MANUAL:
+            ctx.enter_context(tc.manual_schedule())
+
+        xv = x.rearrange("(c p j) k -> c p (j k)", p=P, j=CHUNK_BLOCKS)
+        ov = out.rearrange("(c p j) n -> c p (j n)", p=P, j=CHUNK_BLOCKS)
+
+        wraw = const.tile([P, 4 * K], BF16, name="wraw")
+        for m, w in enumerate((dft_real, dft_imag)):
+            nc.sync.dma_start(
+                out=wraw[:, m * 2 * K : (m + 1) * 2 * K].rearrange("p (h k) -> p h k", h=2),
+                in_=w.rearrange("(h p) k -> p h k", p=P),
+            )
+        xs = []
+        for c in range(CHUNKS):
+            xt = xpool.tile([P, CHUNK_BLOCKS * K], BF16, name="xt")
+            nc.sync.dma_start(out=xt[:], in_=xv[c])
+            xs.append(xt)
+
+        ident = const.tile([P, P], F32, name="ident")
+        make_identity(nc, ident[:])
+        warm = const.tile([P, 1], F32, name="warm")
+        nc.vector.memset(warm[:], 1.0)
+        nc.scalar.activation(out=warm[:], in_=warm[:], func=ACT.Ln)
+
+        def transposes(words, first_block):
+            banks = []
+            for pair in range(GROUP_BLOCKS // 2):
+                tp = tpsum.tile([P, 512], F32, name="tp")
+                for b in range(2):
+                    for u in range(2):
+                        col = (first_block + 2 * pair + b) * WORDS + u * P
+                        slot = (2 * b + u) * P
+                        nc.tensor.transpose(tp[:, slot : slot + P], words[:, col : col + P], ident[:])
+                banks.append(tp)
+            return banks
+
+        def regroup(banks):
+            grouped = gpool.tile([P, GROUP_BLOCKS * P * 4], BF16, name="grouped", align_bytes=64)
+            gw = grouped[:].bitcast(F32)
+            for pair, tp in enumerate(banks):
+                nc.vector.tensor_copy(
+                    out=gw[:, pair * 512 : (pair + 1) * 512].rearrange("p (b r u) -> p b r u", b=2, u=2),
+                    in_=tp[:].rearrange("p (b u r) -> p b r u", b=2, u=2),
+                )
+            return grouped
+
+        def quantise(grouped, codes, scales):
+            nc.vector.quantize_mx(out=codes[:].bitcast(FP8X4), scales=scales[:], in_=grouped[:])
+
+        wcodes = const.tile([P, 2 * N], U32, name="wcodes", align_bytes=64)
+        wscales = const.tile([P, 2 * N], U8, name="wscales", align_bytes=64)
+        quantise(regroup(transposes(wraw[:].bitcast(F32), 0)), wcodes, wscales)
+
+        banks_of = {}
+        grouped_of = {}
+        q_of = {}
+        sq_of = {}
+        o_of = {}
+
+        def stage_t(g):
+            c, h = divmod(g, GROUPS_PER_CHUNK)
+            banks_of[g] = transposes(xs[c][:].bitcast(F32), h * GROUP_BLOCKS)
+
+        def stage_tc(g):
+            grouped_of[g] = regroup(banks_of.pop(g))
+
+        def stage_q(g):
+            codes = qpool.tile([P, GROUP_BLOCKS * P], U32, name="codes", align_bytes=64)
+            scales = qpool.tile([P, GROUP_BLOCKS * P], U8, name="scales", align_bytes=64)
+            quantise(grouped_of.pop(g), codes, scales)
+            q_of[g] = (codes, scales)
+
+        def stage_mx_sq(g):
+            codes, scales = q_of.pop(g)
+            sq = spool.tile([P, GROUP_BLOCKS * 2 * N], F32, name="sq")
+            zs = []
+            for b in range(GROUP_BLOCKS):
+                z = zpsum.tile([P, 2 * N], F32, name="z")
+                nc.tensor.matmul_mx(
+                    out=z[:],
+                    lhsT=codes[:, b * P : (b + 1) * P].bitcast(FP8X4),
+                    lhsT_scale=scales[:, b * P : (b + 1) * P],
+                    rhs=wcodes[:].bitcast(FP8X4),
+                    rhs_scale=wscales[:],
+                    start=True,
+                    stop=True,
+                )
+                zs.append(z)
+            for b, z in enumerate(zs):
+                nc.scalar.activation(out=sq[:, b * 2 * N : (b + 1) * 2 * N], in_=z[:], func=ACT.Square)
+            sq_of[g] = sq
+
+        def stage_add(g):
+            c, h = divmod(g, GROUPS_PER_CHUNK)
+            if h == 0:
+                o_of[c] = opool.tile([P, CHUNK_BLOCKS * N], F32, name="o")
+            o = o_of[c]
+            sqv = sq_of.pop(g)[:].rearrange("p (b m n) -> p b m n", b=GROUP_BLOCKS, m=2)
+            part = o[:, h * GROUP_BLOCKS * N : (h + 1) * GROUP_BLOCKS * N]
+            nc.vector.tensor_tensor(
+                out=part.rearrange("p (b n) -> p b n", b=GROUP_BLOCKS),
+                in0=sqv[:, :, 0, :],
+                in1=sqv[:, :, 1, :],
+                op=ALU.add,
+            )
+
+        def stage_ln(g):
+            c, h = divmod(g, GROUPS_PER_CHUNK)
+            o = o_of[c]
+            part = o[:, h * GROUP_BLOCKS * N : (h + 1) * GROUP_BLOCKS * N]
+            nc.scalar.activation(out=part, in_=part, func=ACT.Ln)
+            if h == GROUPS_PER_CHUNK - 1:
+                nc.sync.dma_start(out=ov[c], in_=o_of.pop(c)[:])
+
+        for i in range(-2, GROUPS + 1):
+            if 0 <= i - 1:
+                stage_add(i - 1)
+            if i + 2 < GROUPS:
+                stage_t(i + 2)
+                stage_tc(i + 2)
+            if 0 <= i + 1 < GROUPS:
+                stage_q(i + 1)
+            if 0 <= i < GROUPS:
+                stage_mx_sq(i)
+            if 0 <= i - 1:
+                stage_ln(i - 1)

@@ -10,37 +10,59 @@ U8 = mybir.dt.uint8
 FP8X4 = mybir.dt.float8_e4m3fn_x4
 ACT = mybir.ActivationFunctionType
 ALU = mybir.AluOpType
+AX = mybir.AxisListType
 
 P = 128
 B, K, N = 16384, 512, 256
 FLOPS = 2 * B * K * 2 * N
 
 CHUNK_BLOCKS = 8
-GROUP_BLOCKS = 4
 CHUNKS = B // (P * CHUNK_BLOCKS)
-GROUPS = B // (P * GROUP_BLOCKS)
-GROUPS_PER_CHUNK = CHUNK_BLOCKS // GROUP_BLOCKS
 WORDS = K // 2
+Z = 2 * N
 
 MANUAL = True
+GADD = 3
+VSQ_EVERY = 2
+VSQ_REDUCE = True
+FIRST = [2, 2, 4]
+LAST = [4, 2, 1, 1]
+SBUFS = 3
+OBUFS = 3
+TBUFS = 4
+ZBUFS = 4
+W_ON_SCALAR = True
 
 
 def tile_dft_kernel(tc, x, dft_real, dft_imag, out):
     nc = tc.nc
     with ExitStack() as ctx:
         const = ctx.enter_context(tc.tile_pool(name="const", bufs=1))
-        xpool = ctx.enter_context(tc.tile_pool(name="xpool", bufs=CHUNKS))
+        xpool = ctx.enter_context(tc.tile_pool(name="xpool", bufs=CHUNKS - 1))
         gpool = ctx.enter_context(tc.tile_pool(name="gpool", bufs=3))
         qpool = ctx.enter_context(tc.tile_pool(name="qpool", bufs=3))
-        spool = ctx.enter_context(tc.tile_pool(name="spool", bufs=3))
-        opool = ctx.enter_context(tc.tile_pool(name="opool", bufs=3))
-        tpsum = ctx.enter_context(tc.psum_pool(name="tpsum", bufs=4))
-        zpsum = ctx.enter_context(tc.psum_pool(name="zpsum", bufs=4))
+        spool = ctx.enter_context(tc.tile_pool(name="spool", bufs=SBUFS))
+        vpool = ctx.enter_context(tc.tile_pool(name="vpool", bufs=2))
+        opool = ctx.enter_context(tc.tile_pool(name="opool", bufs=OBUFS))
+        tpsum = ctx.enter_context(tc.psum_pool(name="tpsum", bufs=TBUFS))
+        zpsum = ctx.enter_context(tc.psum_pool(name="zpsum", bufs=ZBUFS))
         if MANUAL:
             ctx.enter_context(tc.manual_schedule())
 
         xv = x.rearrange("(c p j) k -> c p (j k)", p=P, j=CHUNK_BLOCKS)
         ov = out.rearrange("(c p j) n -> c p (j n)", p=P, j=CHUNK_BLOCKS)
+
+        steps = []
+        for c in range(CHUNKS):
+            sizes = FIRST if c == 0 else (LAST if c == CHUNKS - 1 else [4, 4])
+            j = 0
+            for nb in sizes:
+                steps.append((c, j, nb))
+                j += nb
+            assert j == CHUNK_BLOCKS
+        n_steps = len(steps)
+        full = [s for s in range(n_steps) if steps[s][2] == 4]
+        vsq_steps = set([s for t, s in enumerate(full) if VSQ_EVERY and t % VSQ_EVERY == VSQ_EVERY - 1])
 
         wraw = const.tile([P, 4 * K], BF16, name="wraw")
         for m, w in enumerate((dft_real, dft_imag)):
@@ -48,11 +70,18 @@ def tile_dft_kernel(tc, x, dft_real, dft_imag, out):
                 out=wraw[:, m * 2 * K : (m + 1) * 2 * K].rearrange("p (h k) -> p h k", h=2),
                 in_=w.rearrange("(h p) k -> p h k", p=P),
             )
-        xs = []
-        for c in range(CHUNKS):
+        xsrc = {}
+        half = CHUNK_BLOCKS // 2
+        for h in range(2):
+            xh = const.tile([P, half * K], BF16, name="xh%d" % h)
+            nc.sync.dma_start(out=xh[:], in_=xv[0][:, h * half * K : (h + 1) * half * K])
+            for j in range(half):
+                xsrc[(0, h * half + j)] = (xh, j)
+        for c in range(1, CHUNKS):
             xt = xpool.tile([P, CHUNK_BLOCKS * K], BF16, name="xt")
             nc.sync.dma_start(out=xt[:], in_=xv[c])
-            xs.append(xt)
+            for j in range(CHUNK_BLOCKS):
+                xsrc[(c, j)] = (xt, j)
 
         ident = const.tile([P, P], F32, name="ident")
         make_identity(nc, ident[:])
@@ -60,60 +89,73 @@ def tile_dft_kernel(tc, x, dft_real, dft_imag, out):
         nc.vector.memset(warm[:], 1.0)
         nc.scalar.activation(out=warm[:], in_=warm[:], func=ACT.Ln)
 
-        def transposes(words, first_block):
+        def transposes(blocks):
             banks = []
-            for pair in range(GROUP_BLOCKS // 2):
+            for first in range(0, len(blocks), 2):
+                pair = blocks[first : first + 2]
                 tp = tpsum.tile([P, 512], F32, name="tp")
-                for b in range(2):
+                for b, (src, j) in enumerate(pair):
+                    words = src[:].bitcast(F32)
                     for u in range(2):
-                        col = (first_block + 2 * pair + b) * WORDS + u * P
+                        col = j * WORDS + u * P
                         slot = (2 * b + u) * P
                         nc.tensor.transpose(tp[:, slot : slot + P], words[:, col : col + P], ident[:])
-                banks.append(tp)
+                banks.append((tp, len(pair)))
             return banks
 
-        def regroup(banks):
-            grouped = gpool.tile([P, GROUP_BLOCKS * P * 4], BF16, name="grouped", align_bytes=64)
+        def regroup_bank(grouped, index, bank, on_scalar=False):
+            tp, nb = bank
             gw = grouped[:].bitcast(F32)
-            for pair, tp in enumerate(banks):
-                nc.vector.tensor_copy(
-                    out=gw[:, pair * 512 : (pair + 1) * 512].rearrange("p (b r u) -> p b r u", b=2, u=2),
-                    in_=tp[:].rearrange("p (b u r) -> p b r u", b=2, u=2),
-                )
-            return grouped
+            dst = gw[:, index * 512 : index * 512 + nb * 256].rearrange("p (b r u) -> p b r u", b=nb, u=2)
+            src = tp[:, : nb * 256].rearrange("p (b u r) -> p b r u", b=nb, u=2)
+            if on_scalar:
+                nc.scalar.copy(out=dst, in_=src)
+            else:
+                nc.vector.tensor_copy(out=dst, in_=src)
 
-        def quantise(grouped, codes, scales):
-            nc.vector.quantize_mx(out=codes[:].bitcast(FP8X4), scales=scales[:], in_=grouped[:])
+        def quantise(grouped, codes, scales, nb):
+            nc.vector.quantize_mx(
+                out=codes[:, : nb * P].bitcast(FP8X4), scales=scales[:, : nb * P], in_=grouped[:, : nb * 4 * P]
+            )
 
-        wcodes = const.tile([P, 2 * N], U32, name="wcodes", align_bytes=64)
-        wscales = const.tile([P, 2 * N], U8, name="wscales", align_bytes=64)
-        quantise(regroup(transposes(wraw[:].bitcast(F32), 0)), wcodes, wscales)
+        wcodes = const.tile([P, Z], U32, name="wcodes", align_bytes=64)
+        wscales = const.tile([P, Z], U8, name="wscales", align_bytes=64)
+        wgrouped = const.tile([P, 4 * Z], BF16, name="wgrouped", align_bytes=64)
+        wbanks = transposes([(wraw, j) for j in range(4)])
+        regroup_bank(wgrouped, 0, wbanks[0])
+        regroup_bank(wgrouped, 1, wbanks[1], on_scalar=W_ON_SCALAR)
+        quantise(wgrouped, wcodes, wscales, 4)
 
         banks_of = {}
         grouped_of = {}
         q_of = {}
+        z_of = {}
         sq_of = {}
         o_of = {}
 
-        def stage_t(g):
-            c, h = divmod(g, GROUPS_PER_CHUNK)
-            banks_of[g] = transposes(xs[c][:].bitcast(F32), h * GROUP_BLOCKS)
+        def stage_t(s):
+            c, j0, nb = steps[s]
+            banks_of[s] = transposes([xsrc[(c, j0 + b)] for b in range(nb)])
+            grouped_of[s] = gpool.tile([P, 4 * 4 * P], BF16, name="grouped", align_bytes=64)
 
-        def stage_tc(g):
-            grouped_of[g] = regroup(banks_of.pop(g))
+        def stage_tc(s, index):
+            if index < len(banks_of[s]):
+                regroup_bank(grouped_of[s], index, banks_of[s][index])
 
-        def stage_q(g):
-            codes = qpool.tile([P, GROUP_BLOCKS * P], U32, name="codes", align_bytes=64)
-            scales = qpool.tile([P, GROUP_BLOCKS * P], U8, name="scales", align_bytes=64)
-            quantise(grouped_of.pop(g), codes, scales)
-            q_of[g] = (codes, scales)
+        def stage_q(s):
+            nb = steps[s][2]
+            banks_of.pop(s)
+            codes = qpool.tile([P, 4 * P], U32, name="codes", align_bytes=64)
+            scales = qpool.tile([P, 4 * P], U8, name="scales", align_bytes=64)
+            quantise(grouped_of.pop(s), codes, scales, nb)
+            q_of[s] = (codes, scales)
 
-        def stage_mx_sq(g):
-            codes, scales = q_of.pop(g)
-            sq = spool.tile([P, GROUP_BLOCKS * 2 * N], F32, name="sq")
+        def stage_mx(s):
+            nb = steps[s][2]
+            codes, scales = q_of.pop(s)
             zs = []
-            for b in range(GROUP_BLOCKS):
-                z = zpsum.tile([P, 2 * N], F32, name="z")
+            for b in range(nb):
+                z = zpsum.tile([P, Z], F32, name="z")
                 nc.tensor.matmul_mx(
                     out=z[:],
                     lhsT=codes[:, b * P : (b + 1) * P].bitcast(FP8X4),
@@ -124,41 +166,83 @@ def tile_dft_kernel(tc, x, dft_real, dft_imag, out):
                     stop=True,
                 )
                 zs.append(z)
-            for b, z in enumerate(zs):
-                nc.scalar.activation(out=sq[:, b * 2 * N : (b + 1) * 2 * N], in_=z[:], func=ACT.Square)
-            sq_of[g] = sq
+            z_of[s] = zs
+            sq_of[s] = spool.tile([P, 4 * Z], F32, name="sq")
 
-        def stage_add(g):
-            c, h = divmod(g, GROUPS_PER_CHUNK)
-            if h == 0:
-                o_of[c] = opool.tile([P, CHUNK_BLOCKS * N], F32, name="o")
-            o = o_of[c]
-            sqv = sq_of.pop(g)[:].rearrange("p (b m n) -> p b m n", b=GROUP_BLOCKS, m=2)
-            part = o[:, h * GROUP_BLOCKS * N : (h + 1) * GROUP_BLOCKS * N]
-            nc.vector.tensor_tensor(
-                out=part.rearrange("p (b n) -> p b n", b=GROUP_BLOCKS),
-                in0=sqv[:, :, 0, :],
-                in1=sqv[:, :, 1, :],
+        def stage_sq_scalar(s):
+            nb = steps[s][2]
+            sq = sq_of[s]
+            for b in range(nb - 1 if s in vsq_steps else nb):
+                nc.scalar.activation(out=sq[:, b * Z : (b + 1) * Z], in_=z_of[s][b][:], func=ACT.Square)
+
+        def stage_sq_vector(s):
+            if s in vsq_steps:
+                b = steps[s][2] - 1
+                z = z_of[s][b]
+                dst = sq_of[s][:, b * Z : (b + 1) * Z]
+                if VSQ_REDUCE:
+                    nc.vector.tensor_reduce(
+                        out=dst, in_=z[:].unsqueeze(2).to_broadcast([P, Z, 2]), axis=AX.X, op=ALU.mult
+                    )
+                else:
+                    zc = vpool.tile([P, Z], F32, name="zc")
+                    nc.vector.tensor_copy(out=zc[:], in_=z[:])
+                    nc.vector.tensor_tensor(out=dst, in0=z[:], in1=zc[:], op=ALU.mult)
+            z_of.pop(s)
+
+        def add_part(engine, s, b0, b1):
+            c, j0, nb = steps[s]
+            sqv = sq_of[s][:].rearrange("p (b m n) -> p b m n", b=4, m=2)
+            part = o_of[c][:, (j0 + b0) * N : (j0 + b1) * N]
+            engine.tensor_tensor(
+                out=part.rearrange("p (b n) -> p b n", b=b1 - b0),
+                in0=sqv[:, b0:b1, 0, :],
+                in1=sqv[:, b0:b1, 1, :],
                 op=ALU.add,
             )
 
-        def stage_ln(g):
-            c, h = divmod(g, GROUPS_PER_CHUNK)
-            o = o_of[c]
-            part = o[:, h * GROUP_BLOCKS * N : (h + 1) * GROUP_BLOCKS * N]
-            nc.scalar.activation(out=part, in_=part, func=ACT.Ln)
-            if h == GROUPS_PER_CHUNK - 1:
-                nc.sync.dma_start(out=ov[c], in_=o_of.pop(c)[:])
+        def stage_add_gpsimd(s):
+            c, j0, nb = steps[s]
+            if j0 == 0:
+                o_of[c] = opool.tile([P, CHUNK_BLOCKS * N], F32, name="o")
+            if nb == 4 and GADD:
+                add_part(nc.gpsimd, s, 0, GADD)
 
-        for i in range(-2, GROUPS + 1):
+        def stage_add_vector(s):
+            nb = steps[s][2]
+            b0 = GADD if nb == 4 else 0
+            if b0 < nb:
+                add_part(nc.vector, s, b0, nb)
+            sq_of.pop(s)
+
+        def stage_ln(s):
+            c, j0, nb = steps[s]
+            o = o_of[c]
+            part = o[:, j0 * N : (j0 + nb) * N]
+            nc.scalar.activation(out=part, in_=part, func=ACT.Ln)
+            if c == CHUNKS - 1:
+                nc.sync.dma_start(out=ov[c][:, j0 * N : (j0 + nb) * N], in_=part)
+            elif j0 + nb == CHUNK_BLOCKS:
+                nc.sync.dma_start(out=ov[c], in_=o[:])
+
+        for i in range(-2, n_steps + 1):
             if 0 <= i - 1:
-                stage_add(i - 1)
-            if i + 2 < GROUPS:
+                stage_add_gpsimd(i - 1)
+            if i + 2 < n_steps:
                 stage_t(i + 2)
-                stage_tc(i + 2)
-            if 0 <= i + 1 < GROUPS:
+            if i < 0 and 0 <= i + 1:
                 stage_q(i + 1)
-            if 0 <= i < GROUPS:
-                stage_mx_sq(i)
+            if i + 2 < n_steps:
+                stage_tc(i + 2, 0)
+            if 0 <= i - 1:
+                stage_add_vector(i - 1)
+            if 0 <= i and i + 1 < n_steps:
+                stage_q(i + 1)
+            if i + 2 < n_steps:
+                stage_tc(i + 2, 1)
+            if 0 <= i < n_steps:
+                stage_mx(i)
+                stage_sq_scalar(i)
+                stage_sq_vector(i)
             if 0 <= i - 1:
                 stage_ln(i - 1)

@@ -22,15 +22,17 @@ WORDS = K // 2
 Z = 2 * N
 
 MANUAL = True
-GADD = 3
-VSQ_EVERY = 2
+GADD_PLAIN = 4
+GADD_VSQ = 4
+VSQ_NUM, VSQ_DEN = 1, 1
 VSQ_REDUCE = True
 FIRST = [2, 2, 4]
 LAST = [4, 2, 1, 1]
-SBUFS = 3
-OBUFS = 3
+SBUFS = 4
+OBUFS = 4
 TBUFS = 4
 ZBUFS = 4
+AHEAD = 4
 W_ON_SCALAR = True
 
 
@@ -38,7 +40,7 @@ def tile_dft_kernel(tc, x, dft_real, dft_imag, out):
     nc = tc.nc
     with ExitStack() as ctx:
         const = ctx.enter_context(tc.tile_pool(name="const", bufs=1))
-        xpool = ctx.enter_context(tc.tile_pool(name="xpool", bufs=CHUNKS - 1))
+        xpool = ctx.enter_context(tc.tile_pool(name="xpool", bufs=AHEAD + 1))
         gpool = ctx.enter_context(tc.tile_pool(name="gpool", bufs=3))
         qpool = ctx.enter_context(tc.tile_pool(name="qpool", bufs=3))
         spool = ctx.enter_context(tc.tile_pool(name="spool", bufs=SBUFS))
@@ -62,7 +64,12 @@ def tile_dft_kernel(tc, x, dft_real, dft_imag, out):
             assert j == CHUNK_BLOCKS
         n_steps = len(steps)
         full = [s for s in range(n_steps) if steps[s][2] == 4]
-        vsq_steps = set([s for t, s in enumerate(full) if VSQ_EVERY and t % VSQ_EVERY == VSQ_EVERY - 1])
+        vsq_steps = set([s for t, s in enumerate(full) if (t * VSQ_NUM) % VSQ_DEN < VSQ_NUM])
+
+        def gadd(s):
+            if steps[s][2] != 4:
+                return 0
+            return GADD_VSQ if s in vsq_steps else GADD_PLAIN
 
         wraw = const.tile([P, 4 * K], BF16, name="wraw")
         for m, w in enumerate((dft_real, dft_imag)):
@@ -77,11 +84,15 @@ def tile_dft_kernel(tc, x, dft_real, dft_imag, out):
             nc.sync.dma_start(out=xh[:], in_=xv[0][:, h * half * K : (h + 1) * half * K])
             for j in range(half):
                 xsrc[(0, h * half + j)] = (xh, j)
-        for c in range(1, CHUNKS):
+
+        def load(c):
             xt = xpool.tile([P, CHUNK_BLOCKS * K], BF16, name="xt")
             nc.sync.dma_start(out=xt[:], in_=xv[c])
             for j in range(CHUNK_BLOCKS):
                 xsrc[(c, j)] = (xt, j)
+
+        for c in range(1, AHEAD + 1):
+            load(c)
 
         ident = const.tile([P, P], F32, name="ident")
         make_identity(nc, ident[:])
@@ -205,12 +216,12 @@ def tile_dft_kernel(tc, x, dft_real, dft_imag, out):
             c, j0, nb = steps[s]
             if j0 == 0:
                 o_of[c] = opool.tile([P, CHUNK_BLOCKS * N], F32, name="o")
-            if nb == 4 and GADD:
-                add_part(nc.gpsimd, s, 0, GADD)
+            if gadd(s):
+                add_part(nc.gpsimd, s, 0, gadd(s))
 
         def stage_add_vector(s):
             nb = steps[s][2]
-            b0 = GADD if nb == 4 else 0
+            b0 = gadd(s)
             if b0 < nb:
                 add_part(nc.vector, s, b0, nb)
             sq_of.pop(s)
@@ -224,6 +235,8 @@ def tile_dft_kernel(tc, x, dft_real, dft_imag, out):
                 nc.sync.dma_start(out=ov[c][:, j0 * N : (j0 + nb) * N], in_=part)
             elif j0 + nb == CHUNK_BLOCKS:
                 nc.sync.dma_start(out=ov[c], in_=o[:])
+                if c + AHEAD + 1 < CHUNKS:
+                    load(c + AHEAD + 1)
 
         for i in range(-2, n_steps + 1):
             if 0 <= i - 1:

@@ -23,8 +23,8 @@ Z = 2 * N
 
 MANUAL = True
 GADD_PLAIN = 4
-GADD_VSQ = 4
-VSQ_NUM, VSQ_DEN = 1, 1
+GADD_VSQ = 3
+VSQ_NUM, VSQ_DEN = 3, 4
 VSQ_REDUCE = True
 FIRST = [2, 2, 4]
 LAST = [4, 2, 1, 1]
@@ -33,6 +33,7 @@ OBUFS = 4
 TBUFS = 4
 ZBUFS = 4
 AHEAD = 4
+TAIL_VSQ = [2, 1, 0, 1]
 W_ON_SCALAR = True
 
 
@@ -66,10 +67,14 @@ def tile_dft_kernel(tc, x, dft_real, dft_imag, out):
         full = [s for s in range(n_steps) if steps[s][2] == 4]
         vsq_steps = set([s for t, s in enumerate(full) if (t * VSQ_NUM) % VSQ_DEN < VSQ_NUM])
 
+        vsq_count = dict([(s, 1 if s in vsq_steps else 0) for s in range(n_steps)])
+        for back, count in enumerate(TAIL_VSQ):
+            vsq_count[n_steps - len(TAIL_VSQ) + back] = count
+
         def gadd(s):
             if steps[s][2] != 4:
                 return 0
-            return GADD_VSQ if s in vsq_steps else GADD_PLAIN
+            return min(4 - vsq_count[s], GADD_VSQ) if vsq_count[s] else GADD_PLAIN
 
         wraw = const.tile([P, 4 * K], BF16, name="wraw")
         for m, w in enumerate((dft_real, dft_imag)):
@@ -183,12 +188,12 @@ def tile_dft_kernel(tc, x, dft_real, dft_imag, out):
         def stage_sq_scalar(s):
             nb = steps[s][2]
             sq = sq_of[s]
-            for b in range(nb - 1 if s in vsq_steps else nb):
+            for b in range(nb - vsq_count[s]):
                 nc.scalar.activation(out=sq[:, b * Z : (b + 1) * Z], in_=z_of[s][b][:], func=ACT.Square)
 
         def stage_sq_vector(s):
-            if s in vsq_steps:
-                b = steps[s][2] - 1
+            nb = steps[s][2]
+            for b in range(nb - vsq_count[s], nb):
                 z = z_of[s][b]
                 dst = sq_of[s][:, b * Z : (b + 1) * Z]
                 if VSQ_REDUCE:

@@ -10,257 +10,229 @@ U8 = mybir.dt.uint8
 FP8X4 = mybir.dt.float8_e4m3fn_x4
 ACT = mybir.ActivationFunctionType
 ALU = mybir.AluOpType
-AX = mybir.AxisListType
+AXIS = mybir.AxisListType
 
 P = 128
 B, K, N = 16384, 512, 256
 FLOPS = 2 * B * K * 2 * N
 
-CHUNK_BLOCKS = 8
-CHUNKS = B // (P * CHUNK_BLOCKS)
+PACK = 4
 WORDS = K // 2
 Z = 2 * N
-
-MANUAL = True
-GADD_PLAIN = 4
-GADD_VSQ = 3
-VSQ_NUM, VSQ_DEN = 3, 4
-VSQ_REDUCE = True
-FIRST = [2, 2, 4]
-LAST = [4, 2, 1, 1]
-SBUFS = 4
-OBUFS = 4
-TBUFS = 4
-ZBUFS = 4
+BANK = 512
+CHUNK = 8
+CHUNKS = B // (P * CHUNK)
+STEP = 4
+FIRST_STEPS = (2, 2, 4)
+LAST_STEPS = (4, 2, 2)
 AHEAD = 4
-TAIL_VSQ = [2, 1, 0, 1]
-W_ON_SCALAR = True
+GPSIMD_ADDS = 3
+VECTOR_SQUARES = (5, 8)
 
 
 def tile_dft_kernel(tc, x, dft_real, dft_imag, out):
     nc = tc.nc
     with ExitStack() as ctx:
         const = ctx.enter_context(tc.tile_pool(name="const", bufs=1))
-        xpool = ctx.enter_context(tc.tile_pool(name="xpool", bufs=AHEAD + 1))
-        gpool = ctx.enter_context(tc.tile_pool(name="gpool", bufs=3))
-        qpool = ctx.enter_context(tc.tile_pool(name="qpool", bufs=3))
-        spool = ctx.enter_context(tc.tile_pool(name="spool", bufs=SBUFS))
-        vpool = ctx.enter_context(tc.tile_pool(name="vpool", bufs=2))
-        opool = ctx.enter_context(tc.tile_pool(name="opool", bufs=OBUFS))
-        tpsum = ctx.enter_context(tc.psum_pool(name="tpsum", bufs=TBUFS))
-        zpsum = ctx.enter_context(tc.psum_pool(name="zpsum", bufs=ZBUFS))
-        if MANUAL:
-            ctx.enter_context(tc.manual_schedule())
+        x_pool = ctx.enter_context(tc.tile_pool(name="x_pool", bufs=AHEAD + 1))
+        grouped_pool = ctx.enter_context(tc.tile_pool(name="grouped_pool", bufs=3))
+        mx_pool = ctx.enter_context(tc.tile_pool(name="mx_pool", bufs=3))
+        squares_pool = ctx.enter_context(tc.tile_pool(name="squares_pool", bufs=4))
+        result_pool = ctx.enter_context(tc.tile_pool(name="result_pool", bufs=4))
+        transpose_banks = ctx.enter_context(tc.psum_pool(name="transpose_banks", bufs=4))
+        product_banks = ctx.enter_context(tc.psum_pool(name="product_banks", bufs=4))
+        ctx.enter_context(tc.manual_schedule())
 
-        xv = x.rearrange("(c p j) k -> c p (j k)", p=P, j=CHUNK_BLOCKS)
-        ov = out.rearrange("(c p j) n -> c p (j n)", p=P, j=CHUNK_BLOCKS)
+        x_chunks = x.rearrange("(c p j) k -> c p (j k)", p=P, j=CHUNK)
+        out_chunks = out.rearrange("(c p j) n -> c p (j n)", p=P, j=CHUNK)
 
         steps = []
         for c in range(CHUNKS):
-            sizes = FIRST if c == 0 else (LAST if c == CHUNKS - 1 else [4, 4])
-            j = 0
-            for nb in sizes:
-                steps.append((c, j, nb))
-                j += nb
-            assert j == CHUNK_BLOCKS
+            sizes = (STEP, STEP)
+            if c == 0:
+                sizes = FIRST_STEPS
+            if c == CHUNKS - 1:
+                sizes = LAST_STEPS
+            assert sum(sizes) == CHUNK
+            first = 0
+            for blocks in sizes:
+                steps.append((c, first, blocks))
+                first += blocks
         n_steps = len(steps)
-        full = [s for s in range(n_steps) if steps[s][2] == 4]
-        vsq_steps = set([s for t, s in enumerate(full) if (t * VSQ_NUM) % VSQ_DEN < VSQ_NUM])
 
-        vsq_count = dict([(s, 1 if s in vsq_steps else 0) for s in range(n_steps)])
-        for back, count in enumerate(TAIL_VSQ):
-            vsq_count[n_steps - len(TAIL_VSQ) + back] = count
+        on_vector = {}
+        full_steps = 0
+        for s, (c, first, blocks) in enumerate(steps):
+            on_vector[s] = 0
+            if blocks == STEP:
+                if (full_steps * VECTOR_SQUARES[0]) % VECTOR_SQUARES[1] < VECTOR_SQUARES[0]:
+                    on_vector[s] = 1
+                full_steps += 1
 
-        def gadd(s):
-            if steps[s][2] != 4:
-                return 0
-            return min(4 - vsq_count[s], GADD_VSQ) if vsq_count[s] else GADD_PLAIN
+        def on_gpsimd(s):
+            return GPSIMD_ADDS if steps[s][2] == STEP else 0
 
-        wraw = const.tile([P, 4 * K], BF16, name="wraw")
+        w_raw = const.tile([P, 2 * 2 * K], BF16, name="w_raw")
         for m, w in enumerate((dft_real, dft_imag)):
             nc.sync.dma_start(
-                out=wraw[:, m * 2 * K : (m + 1) * 2 * K].rearrange("p (h k) -> p h k", h=2),
+                out=w_raw[:, m * 2 * K : (m + 1) * 2 * K].rearrange("p (h k) -> p h k", h=2),
                 in_=w.rearrange("(h p) k -> p h k", p=P),
             )
-        xsrc = {}
-        half = CHUNK_BLOCKS // 2
-        for h in range(2):
-            xh = const.tile([P, half * K], BF16, name="xh%d" % h)
-            nc.sync.dma_start(out=xh[:], in_=xv[0][:, h * half * K : (h + 1) * half * K])
-            for j in range(half):
-                xsrc[(0, h * half + j)] = (xh, j)
 
-        def load(c):
-            xt = xpool.tile([P, CHUNK_BLOCKS * K], BF16, name="xt")
-            nc.sync.dma_start(out=xt[:], in_=xv[c])
-            for j in range(CHUNK_BLOCKS):
-                xsrc[(c, j)] = (xt, j)
+        x_block = {}
 
+        def load(c, first, blocks, pool):
+            x_tile = pool.tile([P, blocks * K], BF16, name="x_tile_%d" % blocks)
+            nc.sync.dma_start(out=x_tile[:], in_=x_chunks[c][:, first * K : (first + blocks) * K])
+            for j in range(blocks):
+                x_block[(c, first + j)] = (x_tile, j)
+
+        load(0, 0, CHUNK // 2, x_pool)
+        load(0, CHUNK // 2, CHUNK // 2, x_pool)
         for c in range(1, AHEAD + 1):
-            load(c)
+            load(c, 0, CHUNK, x_pool)
 
-        ident = const.tile([P, P], F32, name="ident")
-        make_identity(nc, ident[:])
-        warm = const.tile([P, 1], F32, name="warm")
-        nc.vector.memset(warm[:], 1.0)
-        nc.scalar.activation(out=warm[:], in_=warm[:], func=ACT.Ln)
+        identity = const.tile([P, P], F32, name="identity")
+        make_identity(nc, identity[:])
+        one = const.tile([P, 1], F32, name="one")
+        nc.vector.memset(one[:], 1.0)
+        nc.scalar.activation(out=one[:], in_=one[:], func=ACT.Ln)
 
-        def transposes(blocks):
+        def transpose(blocks):
             banks = []
-            for first in range(0, len(blocks), 2):
-                pair = blocks[first : first + 2]
-                tp = tpsum.tile([P, 512], F32, name="tp")
-                for b, (src, j) in enumerate(pair):
-                    words = src[:].bitcast(F32)
+            for i in range(0, len(blocks), 2):
+                pair = blocks[i : i + 2]
+                bank = transpose_banks.tile([P, BANK], F32, name="bank")
+                for b, (tile, j) in enumerate(pair):
+                    words = tile[:].bitcast(F32)
                     for u in range(2):
-                        col = j * WORDS + u * P
-                        slot = (2 * b + u) * P
-                        nc.tensor.transpose(tp[:, slot : slot + P], words[:, col : col + P], ident[:])
-                banks.append((tp, len(pair)))
+                        nc.tensor.transpose(
+                            bank[:, (2 * b + u) * P : (2 * b + u + 1) * P],
+                            words[:, j * WORDS + u * P : j * WORDS + (u + 1) * P],
+                            identity[:],
+                        )
+                banks.append((bank, len(pair)))
             return banks
 
-        def regroup_bank(grouped, index, bank, on_scalar=False):
-            tp, nb = bank
-            gw = grouped[:].bitcast(F32)
-            dst = gw[:, index * 512 : index * 512 + nb * 256].rearrange("p (b r u) -> p b r u", b=nb, u=2)
-            src = tp[:, : nb * 256].rearrange("p (b u r) -> p b r u", b=nb, u=2)
-            if on_scalar:
-                nc.scalar.copy(out=dst, in_=src)
-            else:
-                nc.vector.tensor_copy(out=dst, in_=src)
+        def regroup(grouped, index, banks):
+            if index < len(banks):
+                bank, blocks = banks[index]
+                nc.vector.tensor_copy(
+                    out=grouped[:]
+                    .bitcast(F32)[:, index * BANK : index * BANK + blocks * WORDS]
+                    .rearrange("p (b r u) -> p b r u", b=blocks, u=2),
+                    in_=bank[:, : blocks * WORDS].rearrange("p (b u r) -> p b r u", b=blocks, u=2),
+                )
 
-        def quantise(grouped, codes, scales, nb):
+        def quantise(grouped, codes, scales, blocks):
             nc.vector.quantize_mx(
-                out=codes[:, : nb * P].bitcast(FP8X4), scales=scales[:, : nb * P], in_=grouped[:, : nb * 4 * P]
+                out=codes[:, : blocks * P].bitcast(FP8X4),
+                scales=scales[:, : blocks * P],
+                in_=grouped[:, : blocks * P * PACK],
             )
 
-        wcodes = const.tile([P, Z], U32, name="wcodes", align_bytes=64)
-        wscales = const.tile([P, Z], U8, name="wscales", align_bytes=64)
-        wgrouped = const.tile([P, 4 * Z], BF16, name="wgrouped", align_bytes=64)
-        wbanks = transposes([(wraw, j) for j in range(4)])
-        regroup_bank(wgrouped, 0, wbanks[0])
-        regroup_bank(wgrouped, 1, wbanks[1], on_scalar=W_ON_SCALAR)
-        quantise(wgrouped, wcodes, wscales, 4)
+        w_grouped = const.tile([P, Z * PACK], BF16, name="w_grouped", align_bytes=64)
+        w_codes = const.tile([P, Z], U32, name="w_codes", align_bytes=64)
+        w_scales = const.tile([P, Z], U8, name="w_scales", align_bytes=64)
+        w_banks = transpose([(w_raw, j) for j in range(4)])
+        regroup(w_grouped, 0, w_banks)
+        regroup(w_grouped, 1, w_banks)
+        quantise(w_grouped, w_codes, w_scales, 4)
 
         banks_of = {}
         grouped_of = {}
-        q_of = {}
-        z_of = {}
-        sq_of = {}
-        o_of = {}
+        mx_of = {}
+        products_of = {}
+        squares_of = {}
+        result_of = {}
 
-        def stage_t(s):
-            c, j0, nb = steps[s]
-            banks_of[s] = transposes([xsrc[(c, j0 + b)] for b in range(nb)])
-            grouped_of[s] = gpool.tile([P, 4 * 4 * P], BF16, name="grouped", align_bytes=64)
+        def transpose_step(s):
+            c, first, blocks = steps[s]
+            banks_of[s] = transpose([x_block[(c, first + b)] for b in range(blocks)])
+            grouped_of[s] = grouped_pool.tile([P, STEP * P * PACK], BF16, name="grouped", align_bytes=64)
 
-        def stage_tc(s, index):
-            if index < len(banks_of[s]):
-                regroup_bank(grouped_of[s], index, banks_of[s][index])
+        def quantise_step(s):
+            codes = mx_pool.tile([P, STEP * P], U32, name="codes", align_bytes=64)
+            scales = mx_pool.tile([P, STEP * P], U8, name="scales", align_bytes=64)
+            quantise(grouped_of[s], codes, scales, steps[s][2])
+            mx_of[s] = (codes, scales)
 
-        def stage_q(s):
-            nb = steps[s][2]
-            banks_of.pop(s)
-            codes = qpool.tile([P, 4 * P], U32, name="codes", align_bytes=64)
-            scales = qpool.tile([P, 4 * P], U8, name="scales", align_bytes=64)
-            quantise(grouped_of.pop(s), codes, scales, nb)
-            q_of[s] = (codes, scales)
-
-        def stage_mx(s):
-            nb = steps[s][2]
-            codes, scales = q_of.pop(s)
-            zs = []
-            for b in range(nb):
-                z = zpsum.tile([P, Z], F32, name="z")
+        def multiply_step(s):
+            codes, scales = mx_of[s]
+            products_of[s] = []
+            for b in range(steps[s][2]):
+                product = product_banks.tile([P, Z], F32, name="product")
                 nc.tensor.matmul_mx(
-                    out=z[:],
+                    out=product[:],
                     lhsT=codes[:, b * P : (b + 1) * P].bitcast(FP8X4),
                     lhsT_scale=scales[:, b * P : (b + 1) * P],
-                    rhs=wcodes[:].bitcast(FP8X4),
-                    rhs_scale=wscales[:],
+                    rhs=w_codes[:].bitcast(FP8X4),
+                    rhs_scale=w_scales[:],
                     start=True,
                     stop=True,
                 )
-                zs.append(z)
-            z_of[s] = zs
-            sq_of[s] = spool.tile([P, 4 * Z], F32, name="sq")
+                products_of[s].append(product)
 
-        def stage_sq_scalar(s):
-            nb = steps[s][2]
-            sq = sq_of[s]
-            for b in range(nb - vsq_count[s]):
-                nc.scalar.activation(out=sq[:, b * Z : (b + 1) * Z], in_=z_of[s][b][:], func=ACT.Square)
+        def square_step(s):
+            blocks = steps[s][2]
+            squares = squares_pool.tile([P, STEP * Z], F32, name="squares")
+            squares_of[s] = squares
+            for b in range(blocks - on_vector[s]):
+                nc.scalar.activation(
+                    out=squares[:, b * Z : (b + 1) * Z], in_=products_of[s][b][:], func=ACT.Square
+                )
+            for b in range(blocks - on_vector[s], blocks):
+                nc.vector.tensor_reduce(
+                    out=squares[:, b * Z : (b + 1) * Z],
+                    in_=products_of[s][b][:].unsqueeze(2).to_broadcast([P, Z, 2]),
+                    axis=AXIS.X,
+                    op=ALU.mult,
+                )
 
-        def stage_sq_vector(s):
-            nb = steps[s][2]
-            for b in range(nb - vsq_count[s], nb):
-                z = z_of[s][b]
-                dst = sq_of[s][:, b * Z : (b + 1) * Z]
-                if VSQ_REDUCE:
-                    nc.vector.tensor_reduce(
-                        out=dst, in_=z[:].unsqueeze(2).to_broadcast([P, Z, 2]), axis=AX.X, op=ALU.mult
-                    )
-                else:
-                    zc = vpool.tile([P, Z], F32, name="zc")
-                    nc.vector.tensor_copy(out=zc[:], in_=z[:])
-                    nc.vector.tensor_tensor(out=dst, in0=z[:], in1=zc[:], op=ALU.mult)
-            z_of.pop(s)
+        def add(engine, s, b0, b1):
+            c, first, blocks = steps[s]
+            if b0 < b1:
+                halves = squares_of[s][:].rearrange("p (b m n) -> p b m n", b=STEP, m=2)
+                engine.tensor_tensor(
+                    out=result_of[c][:, (first + b0) * N : (first + b1) * N].rearrange(
+                        "p (b n) -> p b n", b=b1 - b0
+                    ),
+                    in0=halves[:, b0:b1, 0, :],
+                    in1=halves[:, b0:b1, 1, :],
+                    op=ALU.add,
+                )
 
-        def add_part(engine, s, b0, b1):
-            c, j0, nb = steps[s]
-            sqv = sq_of[s][:].rearrange("p (b m n) -> p b m n", b=4, m=2)
-            part = o_of[c][:, (j0 + b0) * N : (j0 + b1) * N]
-            engine.tensor_tensor(
-                out=part.rearrange("p (b n) -> p b n", b=b1 - b0),
-                in0=sqv[:, b0:b1, 0, :],
-                in1=sqv[:, b0:b1, 1, :],
-                op=ALU.add,
-            )
-
-        def stage_add_gpsimd(s):
-            c, j0, nb = steps[s]
-            if j0 == 0:
-                o_of[c] = opool.tile([P, CHUNK_BLOCKS * N], F32, name="o")
-            if gadd(s):
-                add_part(nc.gpsimd, s, 0, gadd(s))
-
-        def stage_add_vector(s):
-            nb = steps[s][2]
-            b0 = gadd(s)
-            if b0 < nb:
-                add_part(nc.vector, s, b0, nb)
-            sq_of.pop(s)
-
-        def stage_ln(s):
-            c, j0, nb = steps[s]
-            o = o_of[c]
-            part = o[:, j0 * N : (j0 + nb) * N]
+        def log_step(s):
+            c, first, blocks = steps[s]
+            part = result_of[c][:, first * N : (first + blocks) * N]
             nc.scalar.activation(out=part, in_=part, func=ACT.Ln)
             if c == CHUNKS - 1:
-                nc.sync.dma_start(out=ov[c][:, j0 * N : (j0 + nb) * N], in_=part)
-            elif j0 + nb == CHUNK_BLOCKS:
-                nc.sync.dma_start(out=ov[c], in_=o[:])
+                nc.sync.dma_start(out=out_chunks[c][:, first * N : (first + blocks) * N], in_=part)
+            elif first + blocks == CHUNK:
+                nc.sync.dma_start(out=out_chunks[c], in_=result_of[c][:])
                 if c + AHEAD + 1 < CHUNKS:
-                    load(c + AHEAD + 1)
+                    load(c + AHEAD + 1, 0, CHUNK, x_pool)
 
         for i in range(-2, n_steps + 1):
-            if 0 <= i - 1:
-                stage_add_gpsimd(i - 1)
-            if i + 2 < n_steps:
-                stage_t(i + 2)
-            if i < 0 and 0 <= i + 1:
-                stage_q(i + 1)
-            if i + 2 < n_steps:
-                stage_tc(i + 2, 0)
-            if 0 <= i - 1:
-                stage_add_vector(i - 1)
-            if 0 <= i and i + 1 < n_steps:
-                stage_q(i + 1)
-            if i + 2 < n_steps:
-                stage_tc(i + 2, 1)
+            ahead2, ahead1, behind = i + 2, i + 1, i - 1
+            if behind >= 0:
+                if steps[behind][1] == 0:
+                    result_of[steps[behind][0]] = result_pool.tile([P, CHUNK * N], F32, name="result")
+                add(nc.gpsimd, behind, 0, on_gpsimd(behind))
+            if ahead2 < n_steps:
+                transpose_step(ahead2)
+            if i == -1:
+                quantise_step(ahead1)
+            if ahead2 < n_steps:
+                regroup(grouped_of[ahead2], 0, banks_of[ahead2])
+            if behind >= 0:
+                add(nc.vector, behind, on_gpsimd(behind), steps[behind][2])
+            if 0 <= i and ahead1 < n_steps:
+                quantise_step(ahead1)
+            if ahead2 < n_steps:
+                regroup(grouped_of[ahead2], 1, banks_of[ahead2])
             if 0 <= i < n_steps:
-                stage_mx(i)
-                stage_sq_scalar(i)
-                stage_sq_vector(i)
-            if 0 <= i - 1:
-                stage_ln(i - 1)
+                multiply_step(i)
+                square_step(i)
+            if behind >= 0:
+                log_step(behind)

@@ -25,9 +25,7 @@ CHUNKS = B // (P * CHUNK)
 STEP = 4
 FIRST_STEPS = (2, 2, 4)
 LAST_STEPS = (4, 2, 2)
-AHEAD = 4
-GPSIMD_ADDS = 3
-VECTOR_SQUARES = (5, 8)
+AHEAD = 5
 
 
 def tile_dft_kernel(tc, x, dft_real, dft_imag, out):
@@ -36,10 +34,11 @@ def tile_dft_kernel(tc, x, dft_real, dft_imag, out):
         const = ctx.enter_context(tc.tile_pool(name="const", bufs=1))
         x_pool = ctx.enter_context(tc.tile_pool(name="x_pool", bufs=AHEAD + 1))
         grouped_pool = ctx.enter_context(tc.tile_pool(name="grouped_pool", bufs=3))
-        mx_pool = ctx.enter_context(tc.tile_pool(name="mx_pool", bufs=3))
+        mx_pool = ctx.enter_context(tc.tile_pool(name="mx_pool", bufs=4))
         squares_pool = ctx.enter_context(tc.tile_pool(name="squares_pool", bufs=4))
         result_pool = ctx.enter_context(tc.tile_pool(name="result_pool", bufs=4))
-        transpose_banks = ctx.enter_context(tc.psum_pool(name="transpose_banks", bufs=4))
+        transpose_banks = ctx.enter_context(tc.psum_pool(name="transpose_banks", bufs=2))
+        sum_banks = ctx.enter_context(tc.psum_pool(name="sum_banks", bufs=2))
         product_banks = ctx.enter_context(tc.psum_pool(name="product_banks", bufs=4))
         ctx.enter_context(tc.manual_schedule())
 
@@ -60,17 +59,11 @@ def tile_dft_kernel(tc, x, dft_real, dft_imag, out):
                 first += blocks
         n_steps = len(steps)
 
-        on_vector = {}
-        full_steps = 0
-        for s, (c, first, blocks) in enumerate(steps):
-            on_vector[s] = 0
-            if blocks == STEP:
-                if (full_steps * VECTOR_SQUARES[0]) % VECTOR_SQUARES[1] < VECTOR_SQUARES[0]:
-                    on_vector[s] = 1
-                full_steps += 1
+        def is_column_step(s):
+            return steps[s][2] == STEP and s % 2 == 1
 
-        def on_gpsimd(s):
-            return GPSIMD_ADDS if steps[s][2] == STEP else 0
+        def on_vector(s):
+            return 1 if s >= 2 else 0
 
         w_raw = const.tile([P, 2 * 2 * K], BF16, name="w_raw")
         for m, w in enumerate((dft_real, dft_imag)):
@@ -81,16 +74,17 @@ def tile_dft_kernel(tc, x, dft_real, dft_imag, out):
 
         x_block = {}
 
-        def load(c, first, blocks, pool):
-            x_tile = pool.tile([P, blocks * K], BF16, name="x_tile_%d" % blocks)
+        def load(c, first, blocks):
+            x_tile = x_pool.tile([P, blocks * K], BF16, name="x_tile_%d" % blocks)
             nc.sync.dma_start(out=x_tile[:], in_=x_chunks[c][:, first * K : (first + blocks) * K])
             for j in range(blocks):
                 x_block[(c, first + j)] = (x_tile, j)
 
-        load(0, 0, CHUNK // 2, x_pool)
-        load(0, CHUNK // 2, CHUNK // 2, x_pool)
+        load(0, 0, 2)
+        load(0, 2, 2)
+        load(0, 4, 4)
         for c in range(1, AHEAD + 1):
-            load(c, 0, CHUNK, x_pool)
+            load(c, 0, CHUNK)
 
         identity = const.tile([P, P], F32, name="identity")
         make_identity(nc, identity[:])
@@ -98,63 +92,65 @@ def tile_dft_kernel(tc, x, dft_real, dft_imag, out):
         nc.vector.memset(one[:], 1.0)
         nc.scalar.activation(out=one[:], in_=one[:], func=ACT.Ln)
 
-        def transpose(blocks):
-            banks = []
-            for i in range(0, len(blocks), 2):
-                pair = blocks[i : i + 2]
-                bank = transpose_banks.tile([P, BANK], F32, name="bank")
-                for b, (tile, j) in enumerate(pair):
-                    words = tile[:].bitcast(F32)
-                    for u in range(2):
-                        nc.tensor.transpose(
-                            bank[:, (2 * b + u) * P : (2 * b + u + 1) * P],
-                            words[:, j * WORDS + u * P : j * WORDS + (u + 1) * P],
-                            identity[:],
-                        )
-                banks.append((bank, len(pair)))
-            return banks
+        def transpose(bank, blocks):
+            for b, (tile, j) in enumerate(blocks):
+                words = tile[:].bitcast(F32)
+                for u in range(2):
+                    nc.tensor.transpose(
+                        bank[:, (2 * b + u) * P : (2 * b + u + 1) * P],
+                        words[:, j * WORDS + u * P : j * WORDS + (u + 1) * P],
+                        identity[:],
+                    )
 
-        def regroup(grouped, index, banks):
-            if index < len(banks):
-                bank, blocks = banks[index]
-                nc.vector.tensor_copy(
-                    out=grouped[:]
-                    .bitcast(F32)[:, index * BANK : index * BANK + blocks * WORDS]
-                    .rearrange("p (b r u) -> p b r u", b=blocks, u=2),
-                    in_=bank[:, : blocks * WORDS].rearrange("p (b u r) -> p b r u", b=blocks, u=2),
-                )
+        def regroup(copy, grouped, index, bank, blocks):
+            copy(
+                out=grouped[:]
+                .bitcast(F32)[:, index * BANK : index * BANK + blocks * WORDS]
+                .rearrange("p (b r u) -> p b r u", b=blocks, u=2),
+                in_=bank[:, : blocks * WORDS].rearrange("p (b u r) -> p b r u", b=blocks, u=2),
+            )
 
-        def quantise(grouped, codes, scales, blocks):
+        def quantise(grouped, codes, scales, first, blocks):
             nc.vector.quantize_mx(
-                out=codes[:, : blocks * P].bitcast(FP8X4),
-                scales=scales[:, : blocks * P],
-                in_=grouped[:, : blocks * P * PACK],
+                out=codes[:, first * P : (first + blocks) * P].bitcast(FP8X4),
+                scales=scales[:, first * P : (first + blocks) * P],
+                in_=grouped[:, first * P * PACK : (first + blocks) * P * PACK],
             )
 
         w_grouped = const.tile([P, Z * PACK], BF16, name="w_grouped", align_bytes=64)
         w_codes = const.tile([P, Z], U32, name="w_codes", align_bytes=64)
         w_scales = const.tile([P, Z], U8, name="w_scales", align_bytes=64)
-        w_banks = transpose([(w_raw, j) for j in range(4)])
-        regroup(w_grouped, 0, w_banks)
-        regroup(w_grouped, 1, w_banks)
-        quantise(w_grouped, w_codes, w_scales, 4)
+        for m, copy in enumerate((nc.vector.tensor_copy, nc.scalar.copy)):
+            w_bank = sum_banks.tile([P, BANK], F32, name="sum_bank")
+            transpose(w_bank, [(w_raw, 2 * m), (w_raw, 2 * m + 1)])
+            regroup(copy, w_grouped, m, w_bank, 2)
 
         banks_of = {}
         grouped_of = {}
         mx_of = {}
         products_of = {}
         squares_of = {}
+        sums_of = {}
         result_of = {}
 
         def transpose_step(s):
             c, first, blocks = steps[s]
-            banks_of[s] = transpose([x_block[(c, first + b)] for b in range(blocks)])
+            banks_of[s] = []
+            for i in range(0, blocks, 2):
+                bank = transpose_banks.tile([P, BANK], F32, name="bank")
+                transpose(bank, [x_block[(c, first + i)], x_block[(c, first + i + 1)]])
+                banks_of[s].append(bank)
+
+        def regroup_step(s):
             grouped_of[s] = grouped_pool.tile([P, STEP * P * PACK], BF16, name="grouped", align_bytes=64)
+            copy = nc.scalar.copy if s < 2 else nc.vector.tensor_copy
+            for i, bank in enumerate(banks_of[s]):
+                regroup(copy, grouped_of[s], i, bank, 2)
 
         def quantise_step(s):
             codes = mx_pool.tile([P, STEP * P], U32, name="codes", align_bytes=64)
             scales = mx_pool.tile([P, STEP * P], U8, name="scales", align_bytes=64)
-            quantise(grouped_of[s], codes, scales, steps[s][2])
+            quantise(grouped_of[s], codes, scales, 0, steps[s][2])
             mx_of[s] = (codes, scales)
 
         def multiply_step(s):
@@ -162,26 +158,38 @@ def tile_dft_kernel(tc, x, dft_real, dft_imag, out):
             products_of[s] = []
             for b in range(steps[s][2]):
                 product = product_banks.tile([P, Z], F32, name="product")
-                nc.tensor.matmul_mx(
-                    out=product[:],
-                    lhsT=codes[:, b * P : (b + 1) * P].bitcast(FP8X4),
-                    lhsT_scale=scales[:, b * P : (b + 1) * P],
-                    rhs=w_codes[:].bitcast(FP8X4),
-                    rhs_scale=w_scales[:],
-                    start=True,
-                    stop=True,
-                )
+                if is_column_step(s):
+                    w_cols = slice(b * P, (b + 1) * P)
+                    nc.tensor.matmul_mx(
+                        out=product[:],
+                        lhsT=w_codes[:, w_cols].bitcast(FP8X4),
+                        lhsT_scale=w_scales[:, w_cols],
+                        rhs=codes[:].bitcast(FP8X4),
+                        rhs_scale=scales[:],
+                        start=True,
+                        stop=True,
+                    )
+                else:
+                    rows = slice(b * P, (b + 1) * P)
+                    nc.tensor.matmul_mx(
+                        out=product[:],
+                        lhsT=codes[:, rows].bitcast(FP8X4),
+                        lhsT_scale=scales[:, rows],
+                        rhs=w_codes[:].bitcast(FP8X4),
+                        rhs_scale=w_scales[:],
+                        start=True,
+                        stop=True,
+                    )
                 products_of[s].append(product)
 
         def square_step(s):
-            blocks = steps[s][2]
             squares = squares_pool.tile([P, STEP * Z], F32, name="squares")
             squares_of[s] = squares
-            for b in range(blocks - on_vector[s]):
+            for b in range(on_vector(s), steps[s][2]):
                 nc.scalar.activation(
                     out=squares[:, b * Z : (b + 1) * Z], in_=products_of[s][b][:], func=ACT.Square
                 )
-            for b in range(blocks - on_vector[s], blocks):
+            for b in range(on_vector(s)):
                 nc.vector.tensor_reduce(
                     out=squares[:, b * Z : (b + 1) * Z],
                     in_=products_of[s][b][:].unsqueeze(2).to_broadcast([P, Z, 2]),
@@ -189,50 +197,68 @@ def tile_dft_kernel(tc, x, dft_real, dft_imag, out):
                     op=ALU.mult,
                 )
 
-        def add(engine, s, b0, b1):
+        def add_step(s):
             c, first, blocks = steps[s]
-            if b0 < b1:
-                halves = squares_of[s][:].rearrange("p (b m n) -> p b m n", b=STEP, m=2)
-                engine.tensor_tensor(
-                    out=result_of[c][:, (first + b0) * N : (first + b1) * N].rearrange(
-                        "p (b n) -> p b n", b=b1 - b0
-                    ),
-                    in0=halves[:, b0:b1, 0, :],
-                    in1=halves[:, b0:b1, 1, :],
-                    op=ALU.add,
-                )
+            if first == 0:
+                result_of[c] = result_pool.tile([P, CHUNK * N], F32, name="result")
+            squares = squares_of[s]
+            if is_column_step(s):
+                sums_of[s] = []
+                for i in range(0, blocks, 2):
+                    bank = sum_banks.tile([P, BANK], F32, name="sum_bank")
+                    sums_of[s].append(bank)
+                    for j in range(2):
+                        for h in range(2):
+                            for m in range(2):
+                                start = (2 * m + h) * Z + (i + j) * P
+                                nc.tensor.matmul(
+                                    out=bank[:, j * N + h * P : j * N + (h + 1) * P],
+                                    lhsT=squares[:, start : start + P],
+                                    rhs=identity[:],
+                                    start=(m == 0),
+                                    stop=(m == 1),
+                                    is_transpose=True,
+                                )
+            else:
+                engine = nc.vector if c == CHUNKS - 1 else nc.gpsimd
+                for b in range(blocks):
+                    engine.tensor_tensor(
+                        out=result_of[c][:, (first + b) * N : (first + b + 1) * N],
+                        in0=squares[:, b * Z : b * Z + N],
+                        in1=squares[:, b * Z + N : (b + 1) * Z],
+                        op=ALU.add,
+                    )
 
         def log_step(s):
             c, first, blocks = steps[s]
             part = result_of[c][:, first * N : (first + blocks) * N]
-            nc.scalar.activation(out=part, in_=part, func=ACT.Ln)
+            if is_column_step(s):
+                for i, bank in enumerate(sums_of[s]):
+                    nc.scalar.activation(
+                        out=part[:, i * BANK : (i + 1) * BANK], in_=bank[:], func=ACT.Ln
+                    )
+            else:
+                nc.scalar.activation(out=part, in_=part, func=ACT.Ln)
             if c == CHUNKS - 1:
                 nc.sync.dma_start(out=out_chunks[c][:, first * N : (first + blocks) * N], in_=part)
             elif first + blocks == CHUNK:
                 nc.sync.dma_start(out=out_chunks[c], in_=result_of[c][:])
                 if c + AHEAD + 1 < CHUNKS:
-                    load(c + AHEAD + 1, 0, CHUNK, x_pool)
+                    load(c + AHEAD + 1, 0, CHUNK)
 
-        for i in range(-2, n_steps + 1):
-            ahead2, ahead1, behind = i + 2, i + 1, i - 1
-            if behind >= 0:
-                if steps[behind][1] == 0:
-                    result_of[steps[behind][0]] = result_pool.tile([P, CHUNK * N], F32, name="result")
-                add(nc.gpsimd, behind, 0, on_gpsimd(behind))
-            if ahead2 < n_steps:
-                transpose_step(ahead2)
-            if i == -1:
-                quantise_step(ahead1)
-            if ahead2 < n_steps:
-                regroup(grouped_of[ahead2], 0, banks_of[ahead2])
-            if behind >= 0:
-                add(nc.vector, behind, on_gpsimd(behind), steps[behind][2])
-            if 0 <= i and ahead1 < n_steps:
-                quantise_step(ahead1)
-            if ahead2 < n_steps:
-                regroup(grouped_of[ahead2], 1, banks_of[ahead2])
+        for i in range(-3, n_steps + 2):
             if 0 <= i < n_steps:
                 multiply_step(i)
                 square_step(i)
-            if behind >= 0:
-                log_step(behind)
+            if 0 <= i - 1 < n_steps:
+                add_step(i - 1)
+            if i + 3 < n_steps:
+                transpose_step(i + 3)
+                regroup_step(i + 3)
+            if i == -3:
+                quantise(w_grouped, w_codes, w_scales, 0, 2)
+                quantise(w_grouped, w_codes, w_scales, 2, 2)
+            if 0 <= i + 2 < n_steps:
+                quantise_step(i + 2)
+            if 0 <= i - 2 < n_steps:
+                log_step(i - 2)

@@ -35,8 +35,9 @@ def tile_dft_kernel(tc, x, dft_real, dft_imag, out):
         x_pool = ctx.enter_context(tc.tile_pool(name="x_pool", bufs=AHEAD + 1))
         grouped_pool = ctx.enter_context(tc.tile_pool(name="grouped_pool", bufs=3))
         mx_pool = ctx.enter_context(tc.tile_pool(name="mx_pool", bufs=4))
-        squares_pool = ctx.enter_context(tc.tile_pool(name="squares_pool", bufs=4))
-        result_pool = ctx.enter_context(tc.tile_pool(name="result_pool", bufs=4))
+        raw_pool = ctx.enter_context(tc.tile_pool(name="raw_pool", bufs=2))
+        squares_pool = ctx.enter_context(tc.tile_pool(name="squares_pool", bufs=5))
+        result_pool = ctx.enter_context(tc.tile_pool(name="result_pool", bufs=5))
         transpose_banks = ctx.enter_context(tc.psum_pool(name="transpose_banks", bufs=2))
         sum_banks = ctx.enter_context(tc.psum_pool(name="sum_banks", bufs=2))
         product_banks = ctx.enter_context(tc.psum_pool(name="product_banks", bufs=4))
@@ -59,11 +60,20 @@ def tile_dft_kernel(tc, x, dft_real, dft_imag, out):
                 first += blocks
         n_steps = len(steps)
 
+        def is_step(s):
+            return 0 <= s < n_steps
+
         def is_column_step(s):
             return steps[s][2] == STEP and s % 2 == 1
 
         def on_vector(s):
-            return 1 if s >= 2 else 0
+            return (0 if s < 5 else 1 if s < n_steps - 4 else 2) if steps[s][2] == STEP else (1 if s > 4 else 0)
+
+        def copied(s):
+            return 0
+
+        def on_gpsimd(s):
+            return steps[s][2] == STEP and not is_column_step(s)
 
         w_raw = const.tile([P, 2 * 2 * K], BF16, name="w_raw")
         for m, w in enumerate((dft_real, dft_imag)):
@@ -80,10 +90,11 @@ def tile_dft_kernel(tc, x, dft_real, dft_imag, out):
             for j in range(blocks):
                 x_block[(c, first + j)] = (x_tile, j)
 
-        load(0, 0, 2)
-        load(0, 2, 2)
-        load(0, 4, 4)
-        for c in range(1, AHEAD + 1):
+        for first, blocks in ((0, 2), (2, 2), (4, 2), (6, 2)):
+            load(0, first, blocks)
+        load(1, 0, STEP)
+        load(1, STEP, STEP)
+        for c in range(2, AHEAD + 1):
             load(c, 0, CHUNK)
 
         identity = const.tile([P, P], F32, name="identity")
@@ -130,22 +141,26 @@ def tile_dft_kernel(tc, x, dft_real, dft_imag, out):
         mx_of = {}
         products_of = {}
         squares_of = {}
+        raw_of = {}
         sums_of = {}
         result_of = {}
 
-        def transpose_step(s):
+        def transpose_half(s, half):
             c, first, blocks = steps[s]
-            banks_of[s] = []
-            for i in range(0, blocks, 2):
+            if half == 0:
+                grouped_of[s] = grouped_pool.tile([P, STEP * P * PACK], BF16, name="grouped", align_bytes=64)
+            pair = [x_block[(c, first + j)] for j in range(2 * half, min(2 * half + 2, blocks))]
+            if s < 2:
+                bank = product_banks.tile([P, BANK], F32, name="product")
+            else:
                 bank = transpose_banks.tile([P, BANK], F32, name="bank")
-                transpose(bank, [x_block[(c, first + i)], x_block[(c, first + i + 1)]])
-                banks_of[s].append(bank)
+            transpose(bank, pair)
+            banks_of[(s, half)] = (bank, len(pair))
 
-        def regroup_step(s):
-            grouped_of[s] = grouped_pool.tile([P, STEP * P * PACK], BF16, name="grouped", align_bytes=64)
+        def regroup_half(s, half):
             copy = nc.scalar.copy if s < 2 else nc.vector.tensor_copy
-            for i, bank in enumerate(banks_of[s]):
-                regroup(copy, grouped_of[s], i, bank, 2)
+            bank, blocks = banks_of[(s, half)]
+            regroup(copy, grouped_of[s], half, bank, blocks)
 
         def quantise_step(s):
             codes = mx_pool.tile([P, STEP * P], U32, name="codes", align_bytes=64)
@@ -185,11 +200,14 @@ def tile_dft_kernel(tc, x, dft_real, dft_imag, out):
         def square_step(s):
             squares = squares_pool.tile([P, STEP * Z], F32, name="squares")
             squares_of[s] = squares
-            for b in range(on_vector(s), steps[s][2]):
+            for b in range(on_vector(s) + copied(s), steps[s][2]):
                 nc.scalar.activation(
                     out=squares[:, b * Z : (b + 1) * Z], in_=products_of[s][b][:], func=ACT.Square
                 )
-            for b in range(on_vector(s)):
+            for b in range(copied(s)):
+                raw_of[s] = raw_pool.tile([P, Z], F32, name="raw")
+                nc.vector.tensor_copy(out=raw_of[s][:], in_=products_of[s][b][:])
+            for b in range(copied(s), copied(s) + on_vector(s)):
                 nc.vector.tensor_reduce(
                     out=squares[:, b * Z : (b + 1) * Z],
                     in_=products_of[s][b][:].unsqueeze(2).to_broadcast([P, Z, 2]),
@@ -197,68 +215,112 @@ def tile_dft_kernel(tc, x, dft_real, dft_imag, out):
                     op=ALU.mult,
                 )
 
-        def add_step(s):
-            c, first, blocks = steps[s]
-            if first == 0:
-                result_of[c] = result_pool.tile([P, CHUNK * N], F32, name="result")
-            squares = squares_of[s]
-            if is_column_step(s):
-                sums_of[s] = []
-                for i in range(0, blocks, 2):
-                    bank = sum_banks.tile([P, BANK], F32, name="sum_bank")
-                    sums_of[s].append(bank)
-                    for j in range(2):
-                        for h in range(2):
-                            for m in range(2):
-                                start = (2 * m + h) * Z + (i + j) * P
-                                nc.tensor.matmul(
-                                    out=bank[:, j * N + h * P : j * N + (h + 1) * P],
-                                    lhsT=squares[:, start : start + P],
-                                    rhs=identity[:],
-                                    start=(m == 0),
-                                    stop=(m == 1),
-                                    is_transpose=True,
-                                )
-            else:
-                engine = nc.vector if c == CHUNKS - 1 else nc.gpsimd
-                for b in range(blocks):
-                    engine.tensor_tensor(
-                        out=result_of[c][:, (first + b) * N : (first + b + 1) * N],
-                        in0=squares[:, b * Z : b * Z + N],
-                        in1=squares[:, b * Z + N : (b + 1) * Z],
-                        op=ALU.add,
-                    )
+        def square_raw(s):
+            nc.gpsimd.tensor_tensor(
+                out=squares_of[s][:, :Z], in0=raw_of[s][:], in1=raw_of[s][:], op=ALU.mult
+            )
 
-        def log_step(s):
+        def result(c):
+            if c not in result_of:
+                result_of[c] = result_pool.tile([P, CHUNK * N], F32, name="result")
+            return result_of[c]
+
+        def add(engine, s, b0, b1):
             c, first, blocks = steps[s]
-            part = result_of[c][:, first * N : (first + blocks) * N]
-            if is_column_step(s):
-                for i, bank in enumerate(sums_of[s]):
-                    nc.scalar.activation(
-                        out=part[:, i * BANK : (i + 1) * BANK], in_=bank[:], func=ACT.Ln
-                    )
-            else:
-                nc.scalar.activation(out=part, in_=part, func=ACT.Ln)
+            halves = squares_of[s][:].rearrange("p (b m n) -> p b m n", b=STEP, m=2)
+            engine.tensor_tensor(
+                out=result(c)[:, (first + b0) * N : (first + b1) * N].rearrange("p (b n) -> p b n", b=b1 - b0),
+                in0=halves[:, b0:b1, 0, :],
+                in1=halves[:, b0:b1, 1, :],
+                op=ALU.add,
+            )
+
+        def transpose_back(s, pair):
+            bank = sum_banks.tile([P, BANK], F32, name="sum_bank")
+            sums_of[(s, pair)] = bank
+            for j in range(2):
+                for h in range(2):
+                    for m in range(2):
+                        start = (2 * m + h) * Z + (2 * pair + j) * P
+                        nc.tensor.matmul(
+                            out=bank[:, j * N + h * P : j * N + (h + 1) * P],
+                            lhsT=squares_of[s][:, start : start + P],
+                            rhs=identity[:],
+                            start=(m == 0),
+                            stop=(m == 1),
+                            is_transpose=True,
+                        )
+
+        logged = {}
+
+        def log(s, pair):
+            c, first, blocks = steps[s]
+            cols = slice((first + 2 * pair) * N, (first + 2 * pair + 2) * N)
+            part = result(c)[:, cols]
+            source = sums_of[(s, pair)][:] if is_column_step(s) else part
+            nc.scalar.activation(out=part, in_=source, func=ACT.Ln)
+            logged[s] = logged.get(s, 0) + 2
             if c == CHUNKS - 1:
-                nc.sync.dma_start(out=out_chunks[c][:, first * N : (first + blocks) * N], in_=part)
-            elif first + blocks == CHUNK:
-                nc.sync.dma_start(out=out_chunks[c], in_=result_of[c][:])
-                if c + AHEAD + 1 < CHUNKS:
+                nc.sync.dma_start(out=out_chunks[c][:, cols], in_=part)
+            elif logged[s] == blocks:
+                cols = slice(first * N, (first + blocks) * N)
+                nc.sync.dma_start(out=out_chunks[c][:, cols], in_=result_of[c][:, cols])
+                logged[-1 - c] = logged.get(-1 - c, 0) + blocks
+                if logged[-1 - c] == CHUNK and c + AHEAD + 1 < CHUNKS:
                     load(c + AHEAD + 1, 0, CHUNK)
 
-        for i in range(-3, n_steps + 2):
-            if 0 <= i < n_steps:
+        def transposes_at(i):
+            if i == -1:
+                return [(2, 0)]
+            if i == 0:
+                return [(2, 1)]
+            if i == 1:
+                return [(3, 0), (3, 1)]
+            if i == 2:
+                return [(4, 0), (4, 1), (5, 0), (5, 1)]
+            return [(i + 3, half) for half in range(2) if is_step(i + 3) and 2 * half < steps[i + 3][2]]
+
+        def quantises_at(i):
+            if not (i >= 3):
+                return [i + 2] if i > -3 else []
+            return [s for s in (i + 2, i + 3) if is_step(s)] if i % 2 == 1 else []
+
+        for i in range(-3, n_steps + 4):
+            if is_step(i):
                 multiply_step(i)
                 square_step(i)
-            if 0 <= i - 1 < n_steps:
-                add_step(i - 1)
-            if i + 3 < n_steps:
-                transpose_step(i + 3)
-                regroup_step(i + 3)
+                if copied(i):
+                    square_raw(i)
+                if on_gpsimd(i):
+                    add(nc.gpsimd, i, 0, 1)
+            if is_step(i - 2) and on_gpsimd(i - 2):
+                add(nc.gpsimd, i - 2, 1, STEP)
+            if is_step(i - 1) and steps[i - 1][2] < STEP:
+                add(nc.vector, i - 1, 0, steps[i - 1][2])
+            halves = transposes_at(i)
+            for s, half in halves:
+                transpose_half(s, half)
+            quantises = quantises_at(i)
+            early = quantises if len(halves) > 2 else []
+            for n, (s, half) in enumerate(halves):
+                regroup_half(s, half)
+                if n == 2:
+                    for q in early:
+                        quantise_step(q)
             if i == -3:
                 quantise(w_grouped, w_codes, w_scales, 0, 2)
                 quantise(w_grouped, w_codes, w_scales, 2, 2)
-            if 0 <= i + 2 < n_steps:
-                quantise_step(i + 2)
-            if 0 <= i - 2 < n_steps:
-                log_step(i - 2)
+            for q in quantises:
+                if q not in early:
+                    quantise_step(q)
+            for s, pair in ((i - 1, 0), (i - 2, 1)):
+                if is_step(s) and is_column_step(s):
+                    transpose_back(s, pair)
+            if is_step(i - 2) and steps[i - 2][2] < STEP:
+                log(i - 2, 0)
+            for s, pair in ((i - 2, 0), (i - 3, 1)):
+                if is_step(s) and is_column_step(s):
+                    log(s, pair)
+            for s, pair in ((i - 3, 0), (i - 4, 1)):
+                if is_step(s) and on_gpsimd(s):
+                    log(s, pair)

@@ -25,7 +25,8 @@ CHUNKS = B // (P * CHUNK)
 STEP = 4
 FIRST_STEPS = (2, 2, 4)
 LAST_STEPS = (4, 2, 2)
-AHEAD = 5
+AHEAD = 6
+GROUP = 2
 
 
 def tile_dft_kernel(tc, x, dft_real, dft_imag, out):
@@ -33,10 +34,10 @@ def tile_dft_kernel(tc, x, dft_real, dft_imag, out):
     with ExitStack() as ctx:
         const = ctx.enter_context(tc.tile_pool(name="const", bufs=1))
         x_pool = ctx.enter_context(tc.tile_pool(name="x_pool", bufs=AHEAD + 1))
-        grouped_pool = ctx.enter_context(tc.tile_pool(name="grouped_pool", bufs=3))
-        mx_pool = ctx.enter_context(tc.tile_pool(name="mx_pool", bufs=4))
+        grouped_pool = ctx.enter_context(tc.tile_pool(name="grouped_pool", bufs=GROUP + 2))
+        mx_pool = ctx.enter_context(tc.tile_pool(name="mx_pool", bufs=GROUP + 3))
         raw_pool = ctx.enter_context(tc.tile_pool(name="raw_pool", bufs=2))
-        squares_pool = ctx.enter_context(tc.tile_pool(name="squares_pool", bufs=5))
+        squares_pool = ctx.enter_context(tc.tile_pool(name="squares_pool", bufs=6))
         result_pool = ctx.enter_context(tc.tile_pool(name="result_pool", bufs=5))
         transpose_banks = ctx.enter_context(tc.psum_pool(name="transpose_banks", bufs=2))
         sum_banks = ctx.enter_context(tc.psum_pool(name="sum_banks", bufs=2))
@@ -64,13 +65,13 @@ def tile_dft_kernel(tc, x, dft_real, dft_imag, out):
             return 0 <= s < n_steps
 
         def is_column_step(s):
-            return steps[s][2] == STEP and s % 2 == 1
+            return steps[s][2] == STEP and s % GROUP == GROUP - 1
 
         def on_vector(s):
-            return (0 if s < 5 else 1 if s < n_steps - 4 else 2) if steps[s][2] == STEP else (1 if s > 4 else 0)
+            return (0 if s < 5 else (0 if copied(s) else 1) if s < n_steps - 4 else 2) if steps[s][2] == STEP else (1 if s > 4 else 0)
 
         def copied(s):
-            return 0
+            return 1 if 5 <= s < n_steps - 4 and on_gpsimd(s) else 0
 
         def on_gpsimd(s):
             return steps[s][2] == STEP and not is_column_step(s)
@@ -132,7 +133,7 @@ def tile_dft_kernel(tc, x, dft_real, dft_imag, out):
         w_codes = const.tile([P, Z], U32, name="w_codes", align_bytes=64)
         w_scales = const.tile([P, Z], U8, name="w_scales", align_bytes=64)
         for m, copy in enumerate((nc.vector.tensor_copy, nc.scalar.copy)):
-            w_bank = sum_banks.tile([P, BANK], F32, name="sum_bank")
+            w_bank = product_banks.tile([P, BANK], F32, name="product")
             transpose(w_bank, [(w_raw, 2 * m), (w_raw, 2 * m + 1)])
             regroup(copy, w_grouped, m, w_bank, 2)
 
@@ -172,7 +173,10 @@ def tile_dft_kernel(tc, x, dft_real, dft_imag, out):
             codes, scales = mx_of[s]
             products_of[s] = []
             for b in range(steps[s][2]):
-                product = product_banks.tile([P, Z], F32, name="product")
+                if b < on_vector(s) + copied(s):
+                    product = product_banks.tile([P, Z], F32, name="product")
+                else:
+                    product = product_banks.tile([P, Z], F32, name="product")
                 if is_column_step(s):
                     w_cols = slice(b * P, (b + 1) * P)
                     nc.tensor.matmul_mx(
@@ -197,17 +201,24 @@ def tile_dft_kernel(tc, x, dft_real, dft_imag, out):
                     )
                 products_of[s].append(product)
 
-        def square_step(s):
+        def scalar_squares(s):
             squares = squares_pool.tile([P, STEP * Z], F32, name="squares")
             squares_of[s] = squares
             for b in range(on_vector(s) + copied(s), steps[s][2]):
                 nc.scalar.activation(
                     out=squares[:, b * Z : (b + 1) * Z], in_=products_of[s][b][:], func=ACT.Square
                 )
-            for b in range(copied(s)):
+
+        def vector_squares(s, blocks):
+            squares = squares_of[s]
+            for b in blocks:
+                if b >= copied(s):
+                    continue
                 raw_of[s] = raw_pool.tile([P, Z], F32, name="raw")
                 nc.vector.tensor_copy(out=raw_of[s][:], in_=products_of[s][b][:])
-            for b in range(copied(s), copied(s) + on_vector(s)):
+            for b in blocks:
+                if b < copied(s):
+                    continue
                 nc.vector.tensor_reduce(
                     out=squares[:, b * Z : (b + 1) * Z],
                     in_=products_of[s][b][:].unsqueeze(2).to_broadcast([P, Z, 2]),
@@ -269,32 +280,49 @@ def tile_dft_kernel(tc, x, dft_real, dft_imag, out):
                 if logged[-1 - c] == CHUNK and c + AHEAD + 1 < CHUNKS:
                     load(c + AHEAD + 1, 0, CHUNK)
 
+        def both_halves(s):
+            return [(s, half) for half in range(2) if is_step(s) and 2 * half < steps[s][2]]
+
         def transposes_at(i):
             if i == -1:
                 return [(2, 0)]
             if i == 0:
                 return [(2, 1)]
             if i == 1:
-                return [(3, 0), (3, 1)]
-            if i == 2:
-                return [(4, 0), (4, 1), (5, 0), (5, 1)]
-            return [(i + 3, half) for half in range(2) if is_step(i + 3) and 2 * half < steps[i + 3][2]]
+                return both_halves(3)
+            if 2 <= i < GROUP + 1:
+                return both_halves(2 * i) + both_halves(2 * i + 1)
+            return both_halves(i + 3 if i < 0 else i + GROUP + 1)
 
         def quantises_at(i):
-            if not (i >= 3):
+            if i < 3:
                 return [i + 2] if i > -3 else []
-            return [s for s in (i + 2, i + 3) if is_step(s)] if i % 2 == 1 else []
+            return [s for s in range(i + 2, i + GROUP + 2) if is_step(s)] if i % GROUP == GROUP - 1 else []
 
-        for i in range(-3, n_steps + 4):
+        def log_lag(s):
+            if is_column_step(s):
+                return 2
+            return 3 if s % GROUP == 0 else 4
+
+        for i in range(-3, n_steps + 7):
             if is_step(i):
                 multiply_step(i)
-                square_step(i)
+            for s in range(i - 7, i - 1):
+                if is_step(s) and steps[s][2] == STEP and is_column_step(s):
+                    for pair in range(2):
+                        if s + log_lag(s) + pair == i:
+                            log(s, pair)
+            now = 0
+            if is_step(i):
+                scalar_squares(i)
+                now = 0 if False else on_vector(i) + copied(i)
+                vector_squares(i, range(now))
                 if copied(i):
                     square_raw(i)
-                if on_gpsimd(i):
+                if on_gpsimd(i) and i % GROUP == 0 and not copied(i):
                     add(nc.gpsimd, i, 0, 1)
             if is_step(i - 2) and on_gpsimd(i - 2):
-                add(nc.gpsimd, i - 2, 1, STEP)
+                add(nc.gpsimd, i - 2, 1 if (i - 2) % GROUP == 0 and not copied(i - 2) else 0, STEP)
             if is_step(i - 1) and steps[i - 1][2] < STEP:
                 add(nc.vector, i - 1, 0, steps[i - 1][2])
             halves = transposes_at(i)
@@ -307,6 +335,8 @@ def tile_dft_kernel(tc, x, dft_real, dft_imag, out):
                 if n == 2:
                     for q in early:
                         quantise_step(q)
+            if is_step(i):
+                vector_squares(i, range(now, on_vector(i) + copied(i)))
             if i == -3:
                 quantise(w_grouped, w_codes, w_scales, 0, 2)
                 quantise(w_grouped, w_codes, w_scales, 2, 2)
@@ -318,9 +348,8 @@ def tile_dft_kernel(tc, x, dft_real, dft_imag, out):
                     transpose_back(s, pair)
             if is_step(i - 2) and steps[i - 2][2] < STEP:
                 log(i - 2, 0)
-            for s, pair in ((i - 2, 0), (i - 3, 1)):
-                if is_step(s) and is_column_step(s):
-                    log(s, pair)
-            for s, pair in ((i - 3, 0), (i - 4, 1)):
-                if is_step(s) and on_gpsimd(s):
-                    log(s, pair)
+            for s in range(i - 7, i - 1):
+                if is_step(s) and steps[s][2] == STEP and not is_column_step(s):
+                    for pair in range(2):
+                        if s + log_lag(s) + pair == i:
+                            log(s, pair)

@@ -37,8 +37,8 @@ def tile_dft_kernel(tc, x, dft_real, dft_imag, out):
         grouped_pool = ctx.enter_context(tc.tile_pool(name="grouped_pool", bufs=GROUP + 2))
         mx_pool = ctx.enter_context(tc.tile_pool(name="mx_pool", bufs=GROUP + 3))
         raw_pool = ctx.enter_context(tc.tile_pool(name="raw_pool", bufs=2))
-        squares_pool = ctx.enter_context(tc.tile_pool(name="squares_pool", bufs=6))
-        result_pool = ctx.enter_context(tc.tile_pool(name="result_pool", bufs=5))
+        squares_pool = ctx.enter_context(tc.tile_pool(name="squares_pool", bufs=7))
+        result_pool = ctx.enter_context(tc.tile_pool(name="result_pool", bufs=7))
         transpose_banks = ctx.enter_context(tc.psum_pool(name="transpose_banks", bufs=2))
         sum_banks = ctx.enter_context(tc.psum_pool(name="sum_banks", bufs=2))
         product_banks = ctx.enter_context(tc.psum_pool(name="product_banks", bufs=4))
@@ -68,7 +68,10 @@ def tile_dft_kernel(tc, x, dft_real, dft_imag, out):
             return steps[s][2] == STEP and s % GROUP == GROUP - 1
 
         def on_vector(s):
-            return (0 if s < 5 else (0 if copied(s) else 1) if s < n_steps - 4 else 2) if steps[s][2] == STEP else (1 if s > 4 else 0)
+            return (0 if s < 5 else (0 if copied(s) else 1) if s < n_steps - 3 else 2) if steps[s][2] == STEP else (1 if s > 4 else 0)
+
+        def shared(s):
+            return 128 if 5 < s < n_steps - 3 and s % 2 == 0 else 0
 
         def copied(s):
             return 1 if 5 <= s < n_steps - 4 and on_gpsimd(s) else 0
@@ -76,6 +79,7 @@ def tile_dft_kernel(tc, x, dft_real, dft_imag, out):
         def on_gpsimd(s):
             return steps[s][2] == STEP and not is_column_step(s)
 
+        pins = const.tile([P, n_steps], U32, name="pins")
         w_raw = const.tile([P, 2 * 2 * K], BF16, name="w_raw")
         for m, w in enumerate((dft_real, dft_imag)):
             nc.sync.dma_start(
@@ -86,7 +90,9 @@ def tile_dft_kernel(tc, x, dft_real, dft_imag, out):
         x_block = {}
 
         def load(c, first, blocks):
-            x_tile = x_pool.tile([P, blocks * K], BF16, name="x_tile_%d" % blocks)
+            x_tile = x_pool.tile(
+                [P, blocks * K], BF16, name="x_tile_%d" % blocks, bufs=AHEAD + 1 if blocks == CHUNK else 4
+            )
             nc.sync.dma_start(out=x_tile[:], in_=x_chunks[c][:, first * K : (first + blocks) * K])
             for j in range(blocks):
                 x_block[(c, first + j)] = (x_tile, j)
@@ -98,6 +104,15 @@ def tile_dft_kernel(tc, x, dft_real, dft_imag, out):
         for c in range(2, AHEAD + 1):
             load(c, 0, CHUNK)
 
+        warm = const.tile([P, BANK], BF16, name="warm")
+        nc.vector.memset(warm[:], 0.0)
+
+        def warm_up(count):
+            for n in range(count):
+                bank = transpose_banks.tile([P, BANK], F32, name="bank")
+                nc.tensor.matmul(out=bank[:], lhsT=warm[:, :P], rhs=warm[:], start=True, stop=True)
+
+        warm_up(4)
         identity = const.tile([P, P], F32, name="identity")
         make_identity(nc, identity[:])
         one = const.tile([P, 1], F32, name="one")
@@ -135,6 +150,7 @@ def tile_dft_kernel(tc, x, dft_real, dft_imag, out):
         for m, copy in enumerate((nc.vector.tensor_copy, nc.scalar.copy)):
             w_bank = product_banks.tile([P, BANK], F32, name="product")
             transpose(w_bank, [(w_raw, 2 * m), (w_raw, 2 * m + 1)])
+            warm_up(1)
             regroup(copy, w_grouped, m, w_bank, 2)
 
         banks_of = {}
@@ -205,8 +221,9 @@ def tile_dft_kernel(tc, x, dft_real, dft_imag, out):
             squares = squares_pool.tile([P, STEP * Z], F32, name="squares")
             squares_of[s] = squares
             for b in range(on_vector(s) + copied(s), steps[s][2]):
+                part = shared(s) if b == on_vector(s) + copied(s) else 0
                 nc.scalar.activation(
-                    out=squares[:, b * Z : (b + 1) * Z], in_=products_of[s][b][:], func=ACT.Square
+                    out=squares[:, b * Z + part : (b + 1) * Z], in_=products_of[s][b][:, part:], func=ACT.Square
                 )
 
         def vector_squares(s, blocks):
@@ -222,6 +239,15 @@ def tile_dft_kernel(tc, x, dft_real, dft_imag, out):
                 nc.vector.tensor_reduce(
                     out=squares[:, b * Z : (b + 1) * Z],
                     in_=products_of[s][b][:].unsqueeze(2).to_broadcast([P, Z, 2]),
+                    axis=AXIS.X,
+                    op=ALU.mult,
+                )
+            part = shared(s)
+            b = on_vector(s) + copied(s)
+            if part and len(blocks):
+                nc.vector.tensor_reduce(
+                    out=squares[:, b * Z : b * Z + part],
+                    in_=products_of[s][b][:, :part].unsqueeze(2).to_broadcast([P, part, 2]),
                     axis=AXIS.X,
                     op=ALU.mult,
                 )
@@ -264,13 +290,13 @@ def tile_dft_kernel(tc, x, dft_real, dft_imag, out):
 
         logged = {}
 
-        def log(s, pair):
+        def log(s, pair, pairs=1):
             c, first, blocks = steps[s]
-            cols = slice((first + 2 * pair) * N, (first + 2 * pair + 2) * N)
+            cols = slice((first + 2 * pair) * N, (first + 2 * pair + 2 * pairs) * N)
             part = result(c)[:, cols]
             source = sums_of[(s, pair)][:] if is_column_step(s) else part
             nc.scalar.activation(out=part, in_=source, func=ACT.Ln)
-            logged[s] = logged.get(s, 0) + 2
+            logged[s] = logged.get(s, 0) + 2 * pairs
             if c == CHUNKS - 1:
                 nc.sync.dma_start(out=out_chunks[c][:, cols], in_=part)
             elif logged[s] == blocks:
@@ -302,7 +328,7 @@ def tile_dft_kernel(tc, x, dft_real, dft_imag, out):
         def log_lag(s):
             if is_column_step(s):
                 return 2
-            return 3 if s % GROUP == 0 else 4
+            return 4 if s % GROUP == 0 else 5
 
         for i in range(-3, n_steps + 7):
             if is_step(i):
@@ -317,17 +343,21 @@ def tile_dft_kernel(tc, x, dft_real, dft_imag, out):
                 scalar_squares(i)
                 now = 0 if False else on_vector(i) + copied(i)
                 vector_squares(i, range(now))
-                if copied(i):
-                    square_raw(i)
                 if on_gpsimd(i) and i % GROUP == 0 and not copied(i):
                     add(nc.gpsimd, i, 0, 1)
+            if is_step(i) and copied(i):
+                nc.gpsimd.tensor_copy(out=pins[:, i : i + 1], in_=mx_of[i + 2][0][:, :1])
             if is_step(i - 2) and on_gpsimd(i - 2):
                 add(nc.gpsimd, i - 2, 1 if (i - 2) % GROUP == 0 and not copied(i - 2) else 0, STEP)
+            if is_step(i) and copied(i):
+                square_raw(i)
             if is_step(i - 1) and steps[i - 1][2] < STEP:
                 add(nc.vector, i - 1, 0, steps[i - 1][2])
             halves = transposes_at(i)
             for s, half in halves:
                 transpose_half(s, half)
+                if i < -1:
+                    warm_up(1)
             quantises = quantises_at(i)
             early = quantises if len(halves) > 2 else []
             for n, (s, half) in enumerate(halves):
@@ -350,6 +380,5 @@ def tile_dft_kernel(tc, x, dft_real, dft_imag, out):
                 log(i - 2, 0)
             for s in range(i - 7, i - 1):
                 if is_step(s) and steps[s][2] == STEP and not is_column_step(s):
-                    for pair in range(2):
-                        if s + log_lag(s) + pair == i:
-                            log(s, pair)
+                    if s + log_lag(s) == i:
+                        log(s, 0, 2)

@@ -71,7 +71,7 @@ def tile_dft_kernel(tc, x, dft_real, dft_imag, out):
             return (0 if s < 5 else (0 if copied(s) else 1) if s < n_steps - 3 else 2) if steps[s][2] == STEP else (1 if s > 4 else 0)
 
         def shared(s):
-            return 128 if 5 < s < n_steps - 3 and s % 2 == 0 else 0
+            return (256 if s >= n_steps - 2 else 160) if 5 < s and (s % 2 == 0 or s >= n_steps - 2) else 0
 
         def copied(s):
             return 1 if 5 <= s < n_steps - 4 and on_gpsimd(s) else 0
@@ -112,7 +112,7 @@ def tile_dft_kernel(tc, x, dft_real, dft_imag, out):
                 bank = transpose_banks.tile([P, BANK], F32, name="bank")
                 nc.tensor.matmul(out=bank[:], lhsT=warm[:, :P], rhs=warm[:], start=True, stop=True)
 
-        warm_up(4)
+        warm_up(3)
         identity = const.tile([P, P], F32, name="identity")
         make_identity(nc, identity[:])
         one = const.tile([P, 1], F32, name="one")
@@ -175,7 +175,7 @@ def tile_dft_kernel(tc, x, dft_real, dft_imag, out):
             banks_of[(s, half)] = (bank, len(pair))
 
         def regroup_half(s, half):
-            copy = nc.scalar.copy if s < 2 else nc.vector.tensor_copy
+            copy = nc.scalar.copy if s < 2 or s == 4 else nc.vector.tensor_copy
             bank, blocks = banks_of[(s, half)]
             regroup(copy, grouped_of[s], half, bank, blocks)
 
@@ -328,7 +328,7 @@ def tile_dft_kernel(tc, x, dft_real, dft_imag, out):
         def log_lag(s):
             if is_column_step(s):
                 return 2
-            return 4 if s % GROUP == 0 else 5
+            return 3 if s >= n_steps - 4 else 4
 
         for i in range(-3, n_steps + 7):
             if is_step(i):

@@ -71,7 +71,7 @@ def tile_dft_kernel(tc, x, dft_real, dft_imag, out):
             return (0 if s < 5 else (0 if copied(s) else 1) if s < n_steps - 3 else 2) if steps[s][2] == STEP else (1 if s > 4 else 0)
 
         def shared(s):
-            return (256 if s >= n_steps - 2 else 160) if 5 < s and (s % 2 == 0 or s >= n_steps - 2) else 0
+            return (256 if s >= n_steps - 2 else 96) if 5 < s and (s % 2 == 0 or s >= n_steps - 2) else 0
 
         def copied(s):
             return 1 if 5 <= s < n_steps - 4 and on_gpsimd(s) else 0
@@ -112,7 +112,7 @@ def tile_dft_kernel(tc, x, dft_real, dft_imag, out):
                 bank = transpose_banks.tile([P, BANK], F32, name="bank")
                 nc.tensor.matmul(out=bank[:], lhsT=warm[:, :P], rhs=warm[:], start=True, stop=True)
 
-        warm_up(3)
+        warm_up(4)
         identity = const.tile([P, P], F32, name="identity")
         make_identity(nc, identity[:])
         one = const.tile([P, 1], F32, name="one")

from contextlib import ExitStack

import concourse.mybir as mybir
from concourse.masks import make_identity

F32 = mybir.dt.float32
BF16 = mybir.dt.bfloat16
U32 = mybir.dt.uint32
U8 = mybir.dt.uint8
FP8X4 = mybir.dt.float8_e4m3fn_x4
ACT = mybir.ActivationFunctionType
ALU = mybir.AluOpType
AXIS = mybir.AxisListType

P = 128
B, K, N = 16384, 512, 256
FLOPS = 2 * B * K * 2 * N

PACK = 4
WORDS = K // 2
Z = 2 * N
BANK = 512
CHUNK = 8
CHUNKS = B // (P * CHUNK)
STEP = 4
FIRST_STEPS = (2, 2, 4)
LAST_STEPS = (4, 2, 2)
AHEAD = 6
GROUP = 2


def tile_dft_kernel(tc, x, dft_real, dft_imag, out):
    nc = tc.nc
    with ExitStack() as ctx:
        const = ctx.enter_context(tc.tile_pool(name="const", bufs=1))
        x_pool = ctx.enter_context(tc.tile_pool(name="x_pool", bufs=AHEAD + 1))
        grouped_pool = ctx.enter_context(tc.tile_pool(name="grouped_pool", bufs=GROUP + 2))
        mx_pool = ctx.enter_context(tc.tile_pool(name="mx_pool", bufs=GROUP + 3))
        raw_pool = ctx.enter_context(tc.tile_pool(name="raw_pool", bufs=2))
        squares_pool = ctx.enter_context(tc.tile_pool(name="squares_pool", bufs=7))
        result_pool = ctx.enter_context(tc.tile_pool(name="result_pool", bufs=7))
        transpose_banks = ctx.enter_context(tc.psum_pool(name="transpose_banks", bufs=2))
        sum_banks = ctx.enter_context(tc.psum_pool(name="sum_banks", bufs=2))
        product_banks = ctx.enter_context(tc.psum_pool(name="product_banks", bufs=4))
        ctx.enter_context(tc.manual_schedule())

        x_chunks = x.rearrange("(c p j) k -> c p (j k)", p=P, j=CHUNK)
        out_chunks = out.rearrange("(c p j) n -> c p (j n)", p=P, j=CHUNK)

        steps = []
        for c in range(CHUNKS):
            sizes = (STEP, STEP)
            if c == 0:
                sizes = FIRST_STEPS
            if c == CHUNKS - 1:
                sizes = LAST_STEPS
            assert sum(sizes) == CHUNK
            first = 0
            for blocks in sizes:
                steps.append((c, first, blocks))
                first += blocks
        n_steps = len(steps)

        def is_step(s):
            return 0 <= s < n_steps

        def is_column_step(s):
            return steps[s][2] == STEP and s % GROUP == GROUP - 1

        def on_vector(s):
            return (0 if s < 5 else (0 if copied(s) else 1) if s < n_steps - 3 else 2) if steps[s][2] == STEP else (1 if s > 4 else 0)

        def shared(s):
            return (256 if s >= n_steps - 2 else 96) if 5 < s and (s % 2 == 0 or s >= n_steps - 2) else 0

        def copied(s):
            return 1 if 5 <= s < n_steps - 4 and on_gpsimd(s) else 0

        def on_gpsimd(s):
            return steps[s][2] == STEP and not is_column_step(s)

        pins = const.tile([P, n_steps], U32, name="pins")
        w_raw = const.tile([P, 2 * 2 * K], BF16, name="w_raw")
        for m, w in enumerate((dft_real, dft_imag)):
            nc.sync.dma_start(
                out=w_raw[:, m * 2 * K : (m + 1) * 2 * K].rearrange("p (h k) -> p h k", h=2),
                in_=w.rearrange("(h p) k -> p h k", p=P),
            )

        x_block = {}

        def load(c, first, blocks):
            x_tile = x_pool.tile(
                [P, blocks * K], BF16, name="x_tile_%d" % blocks, bufs=AHEAD + 1 if blocks == CHUNK else 4
            )
            nc.sync.dma_start(out=x_tile[:], in_=x_chunks[c][:, first * K : (first + blocks) * K])
            for j in range(blocks):
                x_block[(c, first + j)] = (x_tile, j)

        for first, blocks in ((0, 2), (2, 2), (4, 2), (6, 2)):
            load(0, first, blocks)
        load(1, 0, STEP)
        load(1, STEP, STEP)
        for c in range(2, AHEAD + 1):
            load(c, 0, CHUNK)

        warm = const.tile([P, BANK], BF16, name="warm")
        nc.vector.memset(warm[:], 0.0)

        def warm_up(count):
            for n in range(count):
                bank = transpose_banks.tile([P, BANK], F32, name="bank")
                nc.tensor.matmul(out=bank[:], lhsT=warm[:, :P], rhs=warm[:], start=True, stop=True)

        warm_up(4)
        identity = const.tile([P, P], F32, name="identity")
        make_identity(nc, identity[:])
        one = const.tile([P, 1], F32, name="one")
        nc.vector.memset(one[:], 1.0)
        nc.scalar.activation(out=one[:], in_=one[:], func=ACT.Ln)

        def transpose(bank, blocks):
            for b, (tile, j) in enumerate(blocks):
                words = tile[:].bitcast(F32)
                for u in range(2):
                    nc.tensor.transpose(
                        bank[:, (2 * b + u) * P : (2 * b + u + 1) * P],
                        words[:, j * WORDS + u * P : j * WORDS + (u + 1) * P],
                        identity[:],
                    )

        def regroup(copy, grouped, index, bank, blocks):
            copy(
                out=grouped[:]
                .bitcast(F32)[:, index * BANK : index * BANK + blocks * WORDS]
                .rearrange("p (b r u) -> p b r u", b=blocks, u=2),
                in_=bank[:, : blocks * WORDS].rearrange("p (b u r) -> p b r u", b=blocks, u=2),
            )

        def quantise(grouped, codes, scales, first, blocks):
            nc.vector.quantize_mx(
                out=codes[:, first * P : (first + blocks) * P].bitcast(FP8X4),
                scales=scales[:, first * P : (first + blocks) * P],
                in_=grouped[:, first * P * PACK : (first + blocks) * P * PACK],
            )

        w_grouped = const.tile([P, Z * PACK], BF16, name="w_grouped", align_bytes=64)
        w_codes = const.tile([P, Z], U32, name="w_codes", align_bytes=64)
        w_scales = const.tile([P, Z], U8, name="w_scales", align_bytes=64)
        for m, copy in enumerate((nc.vector.tensor_copy, nc.scalar.copy)):
            w_bank = product_banks.tile([P, BANK], F32, name="product")
            transpose(w_bank, [(w_raw, 2 * m), (w_raw, 2 * m + 1)])
            warm_up(1)
            regroup(copy, w_grouped, m, w_bank, 2)

        banks_of = {}
        grouped_of = {}
        mx_of = {}
        products_of = {}
        squares_of = {}
        raw_of = {}
        sums_of = {}
        result_of = {}

        def transpose_half(s, half):
            c, first, blocks = steps[s]
            if half == 0:
                grouped_of[s] = grouped_pool.tile([P, STEP * P * PACK], BF16, name="grouped", align_bytes=64)
            pair = [x_block[(c, first + j)] for j in range(2 * half, min(2 * half + 2, blocks))]
            if s < 2:
                bank = product_banks.tile([P, BANK], F32, name="product")
            else:
                bank = transpose_banks.tile([P, BANK], F32, name="bank")
            transpose(bank, pair)
            banks_of[(s, half)] = (bank, len(pair))

        def regroup_half(s, half):
            copy = nc.scalar.copy if s < 2 or s == 4 else nc.vector.tensor_copy
            bank, blocks = banks_of[(s, half)]
            regroup(copy, grouped_of[s], half, bank, blocks)

        def quantise_step(s):
            codes = mx_pool.tile([P, STEP * P], U32, name="codes", align_bytes=64)
            scales = mx_pool.tile([P, STEP * P], U8, name="scales", align_bytes=64)
            quantise(grouped_of[s], codes, scales, 0, steps[s][2])
            mx_of[s] = (codes, scales)

        def multiply_step(s):
            codes, scales = mx_of[s]
            products_of[s] = []
            for b in range(steps[s][2]):
                if b < on_vector(s) + copied(s):
                    product = product_banks.tile([P, Z], F32, name="product")
                else:
                    product = product_banks.tile([P, Z], F32, name="product")
                if is_column_step(s):
                    w_cols = slice(b * P, (b + 1) * P)
                    nc.tensor.matmul_mx(
                        out=product[:],
                        lhsT=w_codes[:, w_cols].bitcast(FP8X4),
                        lhsT_scale=w_scales[:, w_cols],
                        rhs=codes[:].bitcast(FP8X4),
                        rhs_scale=scales[:],
                        start=True,
                        stop=True,
                    )
                else:
                    rows = slice(b * P, (b + 1) * P)
                    nc.tensor.matmul_mx(
                        out=product[:],
                        lhsT=codes[:, rows].bitcast(FP8X4),
                        lhsT_scale=scales[:, rows],
                        rhs=w_codes[:].bitcast(FP8X4),
                        rhs_scale=w_scales[:],
                        start=True,
                        stop=True,
                    )
                products_of[s].append(product)

        def scalar_squares(s):
            squares = squares_pool.tile([P, STEP * Z], F32, name="squares")
            squares_of[s] = squares
            for b in range(on_vector(s) + copied(s), steps[s][2]):
                part = shared(s) if b == on_vector(s) + copied(s) else 0
                nc.scalar.activation(
                    out=squares[:, b * Z + part : (b + 1) * Z], in_=products_of[s][b][:, part:], func=ACT.Square
                )

        def vector_squares(s, blocks):
            squares = squares_of[s]
            for b in blocks:
                if b >= copied(s):
                    continue
                raw_of[s] = raw_pool.tile([P, Z], F32, name="raw")
                nc.vector.tensor_copy(out=raw_of[s][:], in_=products_of[s][b][:])
            for b in blocks:
                if b < copied(s):
                    continue
                nc.vector.tensor_reduce(
                    out=squares[:, b * Z : (b + 1) * Z],
                    in_=products_of[s][b][:].unsqueeze(2).to_broadcast([P, Z, 2]),
                    axis=AXIS.X,
                    op=ALU.mult,
                )
            part = shared(s)
            b = on_vector(s) + copied(s)
            if part and len(blocks):
                nc.vector.tensor_reduce(
                    out=squares[:, b * Z : b * Z + part],
                    in_=products_of[s][b][:, :part].unsqueeze(2).to_broadcast([P, part, 2]),
                    axis=AXIS.X,
                    op=ALU.mult,
                )

        def square_raw(s):
            nc.gpsimd.tensor_tensor(
                out=squares_of[s][:, :Z], in0=raw_of[s][:], in1=raw_of[s][:], op=ALU.mult
            )

        def result(c):
            if c not in result_of:
                result_of[c] = result_pool.tile([P, CHUNK * N], F32, name="result")
            return result_of[c]

        def add(engine, s, b0, b1):
            c, first, blocks = steps[s]
            halves = squares_of[s][:].rearrange("p (b m n) -> p b m n", b=STEP, m=2)
            engine.tensor_tensor(
                out=result(c)[:, (first + b0) * N : (first + b1) * N].rearrange("p (b n) -> p b n", b=b1 - b0),
                in0=halves[:, b0:b1, 0, :],
                in1=halves[:, b0:b1, 1, :],
                op=ALU.add,
            )

        def transpose_back(s, pair):
            bank = sum_banks.tile([P, BANK], F32, name="sum_bank")
            sums_of[(s, pair)] = bank
            for j in range(2):
                for h in range(2):
                    for m in range(2):
                        start = (2 * m + h) * Z + (2 * pair + j) * P
                        nc.tensor.matmul(
                            out=bank[:, j * N + h * P : j * N + (h + 1) * P],
                            lhsT=squares_of[s][:, start : start + P],
                            rhs=identity[:],
                            start=(m == 0),
                            stop=(m == 1),
                            is_transpose=True,
                        )

        logged = {}

        def log(s, pair, pairs=1):
            c, first, blocks = steps[s]
            cols = slice((first + 2 * pair) * N, (first + 2 * pair + 2 * pairs) * N)
            part = result(c)[:, cols]
            source = sums_of[(s, pair)][:] if is_column_step(s) else part
            nc.scalar.activation(out=part, in_=source, func=ACT.Ln)
            logged[s] = logged.get(s, 0) + 2 * pairs
            if c == CHUNKS - 1:
                nc.sync.dma_start(out=out_chunks[c][:, cols], in_=part)
            elif logged[s] == blocks:
                cols = slice(first * N, (first + blocks) * N)
                nc.sync.dma_start(out=out_chunks[c][:, cols], in_=result_of[c][:, cols])
                logged[-1 - c] = logged.get(-1 - c, 0) + blocks
                if logged[-1 - c] == CHUNK and c + AHEAD + 1 < CHUNKS:
                    load(c + AHEAD + 1, 0, CHUNK)

        def both_halves(s):
            return [(s, half) for half in range(2) if is_step(s) and 2 * half < steps[s][2]]

        def transposes_at(i):
            if i == -1:
                return [(2, 0)]
            if i == 0:
                return [(2, 1)]
            if i == 1:
                return both_halves(3)
            if 2 <= i < GROUP + 1:
                return both_halves(2 * i) + both_halves(2 * i + 1)
            return both_halves(i + 3 if i < 0 else i + GROUP + 1)

        def quantises_at(i):
            if i < 3:
                return [i + 2] if i > -3 else []
            return [s for s in range(i + 2, i + GROUP + 2) if is_step(s)] if i % GROUP == GROUP - 1 else []

        def log_lag(s):
            if is_column_step(s):
                return 2
            return 3 if s >= n_steps - 4 else 4

        for i in range(-3, n_steps + 7):
            if is_step(i):
                multiply_step(i)
            for s in range(i - 7, i - 1):
                if is_step(s) and steps[s][2] == STEP and is_column_step(s):
                    for pair in range(2):
                        if s + log_lag(s) + pair == i:
                            log(s, pair)
            now = 0
            if is_step(i):
                scalar_squares(i)
                now = 0 if False else on_vector(i) + copied(i)
                vector_squares(i, range(now))
                if on_gpsimd(i) and i % GROUP == 0 and not copied(i):
                    add(nc.gpsimd, i, 0, 1)
            if is_step(i) and copied(i):
                nc.gpsimd.tensor_copy(out=pins[:, i : i + 1], in_=mx_of[i + 2][0][:, :1])
            if is_step(i - 2) and on_gpsimd(i - 2):
                add(nc.gpsimd, i - 2, 1 if (i - 2) % GROUP == 0 and not copied(i - 2) else 0, STEP)
            if is_step(i) and copied(i):
                square_raw(i)
            if is_step(i - 1) and steps[i - 1][2] < STEP:
                add(nc.vector, i - 1, 0, steps[i - 1][2])
            halves = transposes_at(i)
            for s, half in halves:
                transpose_half(s, half)
                if i < -1:
                    warm_up(1)
            quantises = quantises_at(i)
            early = quantises if len(halves) > 2 else []
            for n, (s, half) in enumerate(halves):
                regroup_half(s, half)
                if n == 2:
                    for q in early:
                        quantise_step(q)
            if is_step(i):
                vector_squares(i, range(now, on_vector(i) + copied(i)))
            if i == -3:
                quantise(w_grouped, w_codes, w_scales, 0, 2)
                quantise(w_grouped, w_codes, w_scales, 2, 2)
            for q in quantises:
                if q not in early:
                    quantise_step(q)
            for s, pair in ((i - 1, 0), (i - 2, 1)):
                if is_step(s) and is_column_step(s):
                    transpose_back(s, pair)
            if is_step(i - 2) and steps[i - 2][2] < STEP:
                log(i - 2, 0)
            for s in range(i - 7, i - 1):
                if is_step(s) and steps[s][2] == STEP and not is_column_step(s):
                    if s + log_lag(s) == i:
                        log(s, 0, 2)
